import numpy as np
import ml_dtypes


def mxq(x, axis, fmt="e4m3"):
    dtype, down = {"e4m3": (ml_dtypes.float8_e4m3fn, 7), "e5m2": (ml_dtypes.float8_e5m2, 14)}[fmt]
    v = np.moveaxis(np.asarray(x, np.float32).astype(ml_dtypes.bfloat16).astype(np.float64), axis, -1)
    blocks = v.reshape(v.shape[:-1] + (-1, 32))
    amax = np.abs(blocks).max(-1, keepdims=True)
    byte = np.maximum(np.where(amax > 0, np.frexp(amax)[1] - 1 + 127, 0) - down, 1)
    scale = np.exp2(byte - 127.0)
    codes = (blocks / scale).astype(np.float32).astype(dtype).astype(np.float64)
    return np.moveaxis((codes * scale).reshape(v.shape), -1, axis)


WIDE = False


def mx_kscale(k):
    if not WIDE:
        return np.ones(k)
    levels = np.array([10, -10, 5, -5, 0])
    a = np.random.permutation(np.resize(levels, k // 512 * 4)).reshape(k // 512, 4)
    idx = np.arange(k)
    return np.exp2(a[idx // 512, idx % 128 // 32])


BF16 = ml_dtypes.bfloat16


def bf(x):
    return np.asarray(x, np.float32).astype(BF16)


def f64(x):
    return np.asarray(x).astype(np.float64)


B, N, D, K = 4, 1024, 1024, 512

BN_EPS = 1e-5
NORM_EPS = 1e-12


def _l2_normalize(v, axis):
    n = np.sqrt(np.sum(v * v, axis=axis, keepdims=True))
    return v / np.maximum(n, NORM_EPS)


def setup_inputs():
    s = mx_kscale(D)
    mu = np.random.standard_normal(D) * 0.125
    h = np.random.standard_normal(K)
    return {"x": bf((np.random.standard_normal((B, N, D)) + mu) * s),
            "clusters": bf((np.random.standard_normal((D, K)) * 0.5 / np.sqrt(D) + mu[:, None] * h * 0.25 / np.sum(mu * mu)) / s[:, None]),
            "clusters2": bf((mu[:, None] + np.random.standard_normal((1, D, K)) / np.sqrt(D)) * s[:, None]),
            "bn_gamma": bf(1.0 + 0.1 * np.random.standard_normal(K)),
            "bn_beta": bf(0.5 * np.random.standard_normal(K))}


def reference(x, clusters, clusters2, bn_gamma, bn_beta):
    x, clusters, clusters2 = f64(x), f64(clusters), f64(clusters2)
    bn_gamma, bn_beta = f64(bn_gamma), f64(bn_beta)
    B, N, D = x.shape
    K = clusters2.shape[-1]
    x_flat = x.reshape(-1, D)
    assignment = mxq(x_flat, 1, "e4m3") @ mxq(clusters, 0, "e4m3")
    mean = np.mean(assignment, axis=0)
    var = np.var(assignment, axis=0)
    assignment = (assignment - mean) * (1.0 / np.sqrt(var + BN_EPS)) * bn_gamma + bn_beta
    e = np.exp(assignment - assignment.max(axis=1, keepdims=True))
    assignment = (e / e.sum(axis=1, keepdims=True))[:, :K]
    assignment = assignment.reshape(B, N, K)
    a_sum = np.sum(assignment, axis=1, keepdims=True)
    a = a_sum * clusters2
    vlad = (mxq(x, 1, "e4m3").transpose(0, 2, 1) @ mxq(assignment, 1, "e4m3")) - a
    vlad = _l2_normalize(vlad, axis=1)
    vlad = vlad.reshape(B, D * K)
    vlad = _l2_normalize(vlad, axis=1)
    return vlad

@@ -1,0 +1,467 @@
+from contextlib import ExitStack
+
+import concourse.mybir as mybir
+from concourse.masks import make_identity
+
+F32 = mybir.dt.float32
+BF16 = mybir.dt.bfloat16
+U32 = mybir.dt.uint32
+U8 = mybir.dt.uint8
+FP8X4 = mybir.dt.float8_e4m3fn_x4
+ALU = mybir.AluOpType
+ACT = mybir.ActivationFunctionType
+AXIS_X = mybir.AxisListType.X
+
+P = 128
+PACK = 4
+K_PASS = P * PACK
+B, N, D, K = 4, 1024, 1024, 512
+ROWS = B * N
+CHUNK = K_PASS
+CHUNKS = ROWS // CHUNK
+CHUNKS_PER_BATCH = N // CHUNK
+D_PASSES = D // K_PASS
+KC = K // P
+D_TILES = D // P
+BANK = 512
+BN_EPS = 1e-5
+NORM_EPS = 1e-12
+
+FLOPS = 2 * ROWS * D * K * 2
+
+
+def tile_modelnew_t_kernel(tc, x, clusters, clusters2, bn_gamma, bn_beta, out):
+    nc = tc.nc
+    with ExitStack() as ctx:
+        ctx.enter_context(tc.manual_schedule())
+        keep = ctx.enter_context(tc.tile_pool(name="keep", bufs=1))
+        wide = ctx.enter_context(tc.tile_pool(name="wide", bufs=2 * CHUNKS))
+        scrap = ctx.enter_context(tc.tile_pool(name="scrap", bufs=2))
+        psum = ctx.enter_context(tc.psum_pool(name="psum", bufs=1))
+
+        def transpose_bank(shape, dtype):
+            return psum.tile(shape, dtype, tag="transposed", name="transposed", bufs=4)
+
+        def sum_bank():
+            return psum.tile([P, BANK], F32, tag="mx_sum", name="mx_sum", bufs=3)
+
+        def copy_out(on_vector, out_ap, in_ap):
+            if on_vector:
+                nc.vector.tensor_copy(out=out_ap, in_=in_ap)
+            else:
+                nc.scalar.copy(out=out_ap, in_=in_ap)
+
+        ident_f = keep.tile([P, P], F32)
+        make_identity(nc, ident_f[:])
+        ident_b = keep.tile([P, P], BF16)
+        make_identity(nc, ident_b[:])
+        ones_f = keep.tile([P, P], F32)
+        nc.vector.memset(ones_f[:], 1.0)
+        neg_half = keep.tile([P, KC], F32)
+        nc.vector.memset(neg_half[:], -0.5)
+        warm = keep.tile([P, 1], F32)
+        nc.vector.memset(warm[:], 0.0)
+        nc.scalar.activation(out=warm[:], in_=warm[:], func=ACT.Exp)
+
+        xn_codes = [keep.tile([P, D], U32, name="xn_codes%d" % ch, align_bytes=64) for ch in range(CHUNKS)]
+        xn_scales = [keep.tile([P, D], U8, name="xn_scales%d" % ch, align_bytes=64) for ch in range(CHUNKS)]
+        c2T = keep.tile([P, KC, D], BF16)
+        sum_a = keep.tile([P, KC, CHUNKS], F32)
+        sum_aa = keep.tile([P, KC, CHUNKS], F32)
+        gamma_beta = keep.tile([P, 2 * KC], F32)
+        mean = keep.tile([P, KC], F32)
+        mean_aa = keep.tile([P, KC], F32)
+        var = keep.tile([P, KC], F32)
+        rstd = keep.tile([P, KC], F32)
+        bn_scale = keep.tile([P, KC], F32)
+        bn_shift = keep.tile([P, KC], F32)
+        neg_a_sum = keep.tile([P, B, KC], F32)
+        small = psum.tile([P, BANK], F32, tag="small")
+        TOTALS = B * KC
+
+        a_sb = {}
+
+        def a_view(ch, kc):
+            return a_sb[ch, kc // 2][:, kc % 2, :]
+
+        with tc.tile_pool(name="stage1", bufs=2) as stage1:
+            x_tiles = {}
+            xd_grouped = {}
+            xd_codes = {}
+            xd_scales = {}
+            xn_grouped = {}
+            X_BUFS = 4
+
+            def load_chunk(ch):
+                b, c = divmod(ch, CHUNKS_PER_BATCH)
+                x_tiles[ch] = stage1.tile([P, PACK * D], BF16, tag="x_sb", name="x_sb", bufs=X_BUFS)
+                rows = x[b, c * CHUNK : (c + 1) * CHUNK, :]
+                nc.sync.dma_start(out=x_tiles[ch][:], in_=rows.rearrange("(q j) d -> q (j d)", j=PACK))
+
+            def transpose_chunk(ch):
+                x_words = x_tiles[ch][:].bitcast(F32)
+                xd_grouped[ch] = stage1.tile(
+                    [P, D_PASSES * CHUNK * PACK], BF16, tag="xd_grouped", name="xd_grouped", align_bytes=64
+                )
+                xd_words = xd_grouped[ch][:].bitcast(F32).rearrange("q (g n u) -> q g n u", g=D_PASSES, u=2)
+                for j in range(PACK):
+                    xt = transpose_bank([P, BANK], F32)
+                    for h in range(2 * D_PASSES):
+                        first = j * (D // 2) + h * P
+                        nc.tensor.transpose(xt[:, h * P : (h + 1) * P], x_words[:, first : first + P], ident_f[:])
+                    copy_out(
+                        j % 2 == 1,
+                        xd_words[:, :, j * P : (j + 1) * P, :],
+                        xt[:].rearrange("q (g u n) -> q g n u", g=D_PASSES, u=2),
+                    )
+
+            def quantise_xd(ch):
+                xd_codes[ch] = stage1.tile(
+                    [P, D_PASSES * CHUNK], U32, tag="xd_codes", name="xd_codes", align_bytes=64
+                )
+                xd_scales[ch] = stage1.tile(
+                    [P, D_PASSES * CHUNK], U8, tag="xd_scales", name="xd_scales", align_bytes=64
+                )
+                nc.vector.quantize_mx(
+                    out=xd_codes[ch][:].bitcast(FP8X4), scales=xd_scales[ch][:], in_=xd_grouped[ch][:]
+                )
+
+            def first_matmul(ch):
+                for kc in range(KC):
+                    if kc % 2 == 0:
+                        a_sb[ch, kc // 2] = wide.tile([P, 2, CHUNK], F32, tag="wide", name="a_sb")
+                    acc = sum_bank()
+                    for g in range(D_PASSES):
+                        k_cols = slice(g * K + kc * P, g * K + (kc + 1) * P)
+                        n_cols = slice(g * CHUNK, (g + 1) * CHUNK)
+                        nc.tensor.matmul_mx(
+                            out=acc[:],
+                            lhsT=c_codes[:, k_cols].bitcast(FP8X4),
+                            lhsT_scale=c_scales[:, k_cols],
+                            rhs=xd_codes[ch][:, n_cols].bitcast(FP8X4),
+                            rhs_scale=xd_scales[ch][:, n_cols],
+                            start=(g == 0),
+                            stop=(g == D_PASSES - 1),
+                        )
+                    nc.scalar.activation(
+                        out=a_view(ch, kc), in_=acc[:], func=ACT.Identity, accum_out=sum_a[:, kc, ch : ch + 1]
+                    )
+                    squares = scrap.tile([P, D], BF16, tag="squares")
+                    nc.scalar.activation(
+                        out=squares[:, 0:CHUNK], in_=acc[:], func=ACT.Square, accum_out=sum_aa[:, kc, ch : ch + 1]
+                    )
+
+            def regroup_xn(ch):
+                xn_grouped[ch] = stage1.tile([P, D * PACK], BF16, tag="xn_grouped", name="xn_grouped", align_bytes=64)
+                nc.vector.tensor_copy(
+                    out=xn_grouped[ch][:].rearrange("q (s i j) -> q s j i", i=4, j=PACK),
+                    in_=x_tiles[ch][:].rearrange("q (j s i) -> q s j i", j=PACK, i=4),
+                )
+
+            def quantise_xn(ch):
+                nc.vector.quantize_mx(
+                    out=xn_codes[ch][:].bitcast(FP8X4), scales=xn_scales[ch][:], in_=xn_grouped[ch][:]
+                )
+
+            load_chunk(0)
+            c_raw = stage1.tile([P, 2 * D_PASSES, 2, K], BF16, bufs=1)
+            nc.sync.dma_start(
+                out=c_raw[:], in_=clusters.rearrange("(h q e) k -> q h e k", h=2 * D_PASSES, e=2)
+            )
+            for ch in range(1, X_BUFS):
+                load_chunk(ch)
+            gb_rows = stage1.tile([P, P], BF16, bufs=1)
+            nc.vector.memset(gb_rows[:], 0.0)
+            nc.sync.dma_start(out=gb_rows[0:KC, :], in_=bn_gamma.rearrange("(r k) -> r k", k=P))
+            nc.sync.dma_start(out=gb_rows[KC : 2 * KC, :], in_=bn_beta.rearrange("(r k) -> r k", k=P))
+
+            transpose_chunk(0)
+            c_grouped = stage1.tile([P, D_PASSES, K, PACK], BF16, bufs=1, align_bytes=64)
+            for g in range(D_PASSES):
+                nc.vector.tensor_copy(
+                    out=c_grouped[:, g].rearrange("q k (u e) -> q k u e", e=2),
+                    in_=c_raw[:, 2 * g : 2 * g + 2].rearrange("q u e k -> q k u e"),
+                )
+            quantise_xd(0)
+            c_codes = stage1.tile([P, D_PASSES * K], U32, bufs=1, align_bytes=64)
+            c_scales = stage1.tile([P, D_PASSES * K], U8, bufs=1, align_bytes=64)
+            nc.vector.quantize_mx(
+                out=c_codes[:].bitcast(FP8X4),
+                scales=c_scales[:],
+                in_=c_grouped[:].rearrange("q g k t -> q (g k t)"),
+            )
+
+            for ch in range(CHUNKS):
+                if ch + 1 < CHUNKS:
+                    transpose_chunk(ch + 1)
+                first_matmul(ch)
+                regroup_xn(ch)
+                if ch + 1 < CHUNKS:
+                    quantise_xd(ch + 1)
+                quantise_xn(ch)
+                if ch + X_BUFS < CHUNKS:
+                    load_chunk(ch + X_BUFS)
+
+            gb_ps = transpose_bank([P, P], BF16)
+            nc.tensor.transpose(gb_ps[:], gb_rows[:], ident_b[:])
+            nc.vector.tensor_copy(out=gamma_beta[:], in_=gb_ps[:, 0 : 2 * KC])
+
+            c2_raw = stage1.tile([P, D_TILES, K], BF16, bufs=1)
+            nc.sync.dma_start(out=c2_raw[:], in_=clusters2[0].rearrange("(t q) k -> q t k", q=P))
+            for kc in range(KC):
+                c2_ps = transpose_bank([P, D], BF16)
+                for t in range(D_TILES):
+                    nc.tensor.transpose(
+                        c2_ps[:, t * P : (t + 1) * P], c2_raw[:, t, kc * P : (kc + 1) * P], ident_b[:]
+                    )
+                nc.scalar.copy(out=c2T[:, kc, :], in_=c2_ps[:])
+
+        nc.vector.tensor_reduce(out=mean[:], in_=sum_a[:], axis=AXIS_X, op=ALU.add)
+        nc.vector.tensor_reduce(out=mean_aa[:], in_=sum_aa[:], axis=AXIS_X, op=ALU.add)
+        nc.vector.tensor_scalar(out=mean[:], in0=mean[:], scalar1=1.0 / ROWS, scalar2=None, op0=ALU.mult)
+        nc.vector.tensor_tensor(out=var[:], in0=mean[:], in1=mean[:], op=ALU.mult)
+        nc.vector.scalar_tensor_tensor(
+            out=var[:], in0=mean_aa[:], scalar=1.0 / ROWS, in1=var[:], op0=ALU.mult, op1=ALU.subtract
+        )
+        nc.vector.tensor_scalar(out=var[:], in0=var[:], scalar1=0.0, scalar2=BN_EPS, op0=ALU.max, op1=ALU.add)
+        nc.gpsimd.tensor_tensor(out=rstd[:], in0=var[:], in1=neg_half[:], op=ALU.pow)
+        nc.vector.tensor_tensor(out=bn_scale[:], in0=gamma_beta[:, 0:KC], in1=rstd[:], op=ALU.mult)
+        nc.vector.tensor_tensor(out=bn_shift[:], in0=mean[:], in1=bn_scale[:], op=ALU.mult)
+        nc.vector.tensor_tensor(out=bn_shift[:], in0=gamma_beta[:, KC : 2 * KC], in1=bn_shift[:], op=ALU.subtract)
+
+        stage2 = ctx.enter_context(tc.tile_pool(name="stage2", bufs=2, reuse_waits="tile"))
+        zt = {}
+        e = {}
+        neg_max = {}
+        row_sum = {}
+        recip = {}
+        p_grouped = {}
+        p_codes = {}
+        p_scales = {}
+        a_sum_ps = {}
+        a_sum_sb = {}
+
+        def normalise(ch):
+            for kc in range(KC):
+                nc.scalar.activation(
+                    out=a_view(ch, kc),
+                    in_=a_view(ch, kc),
+                    func=ACT.Identity,
+                    scale=bn_scale[:, kc : kc + 1],
+                    bias=bn_shift[:, kc : kc + 1],
+                )
+
+        def transpose_z(ch):
+            for j in range(PACK):
+                zt[ch, j] = transpose_bank([P, K], F32)
+                for kc in range(KC):
+                    nc.tensor.transpose(
+                        zt[ch, j][:, kc * P : (kc + 1) * P], a_view(ch, kc)[:, j * P : (j + 1) * P], ident_f[:]
+                    )
+
+        def exponentials(ch):
+            e[ch] = stage2.tile([P, PACK, K], F32, tag="e", name="e")
+            neg_max[ch] = stage2.tile([P, PACK], F32, tag="neg_max", name="neg_max")
+            row_sum[ch] = stage2.tile([P, PACK], F32, tag="row_sum", name="row_sum")
+            for j in range(PACK):
+                nc.vector.tensor_reduce(
+                    out=neg_max[ch][:, j : j + 1], in_=zt[ch, j][:], axis=AXIS_X, op=ALU.max, negate=True
+                )
+                nc.scalar.activation(
+                    out=e[ch][:, j, :],
+                    in_=zt[ch, j][:],
+                    func=ACT.Exp,
+                    bias=neg_max[ch][:, j : j + 1],
+                    scale=1.0,
+                    accum_out=row_sum[ch][:, j : j + 1],
+                )
+
+        def sum_p(ch):
+            b, c = divmod(ch, CHUNKS_PER_BATCH)
+            if c == 0:
+                a_sum_ps[b] = sum_bank()
+            for j in range(PACK):
+                nc.tensor.matmul(
+                    out=a_sum_ps[b][:],
+                    lhsT=recip[ch][:, j : j + 1].to_broadcast([P, P]),
+                    rhs=e[ch][:, j, :],
+                    start=(c == 0 and j == 0),
+                    stop=(c == CHUNKS_PER_BATCH - 1 and j == PACK - 1),
+                )
+
+        def copy_a_sum(b):
+            a_sum_sb[b] = stage2.tile([P, K], F32, tag="a_sum_sb", name="a_sum_sb")
+            nc.scalar.copy(out=a_sum_sb[b][:], in_=a_sum_ps[b][:])
+
+        def turn_a_sum(b):
+            for kc in range(KC):
+                nc.tensor.matmul(
+                    out=small[:, b * KC + kc : b * KC + kc + 1],
+                    lhsT=a_sum_sb[b][:, kc * P : (kc + 1) * P],
+                    rhs=ident_f[:, 0:1],
+                    start=True,
+                    stop=True,
+                )
+
+        def negate_a_sum(b):
+            nc.vector.tensor_scalar(
+                out=neg_a_sum[:, b, :], in0=small[:, b * KC : (b + 1) * KC], scalar1=-1.0, scalar2=None, op0=ALU.mult
+            )
+
+        def round_p(ch):
+            p_grouped[ch] = stage2.tile([P, K, PACK], BF16, tag="p_grouped", name="p_grouped", align_bytes=64)
+            nc.vector.tensor_tensor(
+                out=p_grouped[ch][:],
+                in0=e[ch][:].rearrange("q j k -> q k j"),
+                in1=recip[ch][:].unsqueeze(1).to_broadcast([P, K, PACK]),
+                op=ALU.mult,
+            )
+
+        def quantise_p(ch):
+            p_codes[ch] = stage2.tile([P, K], U32, tag="p_codes", name="p_codes", bufs=CHUNKS, align_bytes=64)
+            p_scales[ch] = stage2.tile([P, K], U8, tag="p_scales", name="p_scales", bufs=CHUNKS, align_bytes=64)
+            nc.vector.quantize_mx(
+                out=p_codes[ch][:].bitcast(FP8X4),
+                scales=p_scales[ch][:],
+                in_=p_grouped[ch][:].rearrange("q k j -> q (k j)"),
+            )
+
+        normalise(0)
+        normalise(1)
+        transpose_z(0)
+        for ch in range(CHUNKS):
+            summed = ch // CHUNKS_PER_BATCH - 1 if ch % CHUNKS_PER_BATCH == 0 else -1
+            exponentials(ch)
+            if summed >= 0:
+                copy_a_sum(summed)
+            if ch > 0:
+                quantise_p(ch - 1)
+            recip[ch] = stage2.tile([P, PACK], F32, tag="recip", name="recip")
+            nc.vector.reciprocal(out=recip[ch][:], in_=row_sum[ch][:])
+            if ch + 1 < CHUNKS:
+                transpose_z(ch + 1)
+            if summed >= 0:
+                turn_a_sum(summed)
+            sum_p(ch)
+            round_p(ch)
+            if summed >= 0:
+                negate_a_sum(summed)
+            if ch + 2 < CHUNKS:
+                normalise(ch + 2)
+        copy_a_sum(B - 1)
+        turn_a_sum(B - 1)
+        quantise_p(CHUNKS - 1)
+        negate_a_sum(B - 1)
+
+        v = {}
+        sum_vv = {}
+        inv_norm = {}
+        unit_sum = {}
+        inv_total = {}
+        factor = {}
+        out_rows = {}
+        HALF_TILES = D_TILES // 2
+
+        def second_matmul(b, kc):
+            v[b, kc] = wide.tile([P, D], F32, tag="wide", name="v")
+            for half in range(D // BANK):
+                d_cols = slice(half * BANK, (half + 1) * BANK)
+                acc = sum_bank()
+                for c in range(CHUNKS_PER_BATCH):
+                    ch = b * CHUNKS_PER_BATCH + c
+                    k_cols = slice(kc * P, (kc + 1) * P)
+                    nc.tensor.matmul_mx(
+                        out=acc[:],
+                        lhsT=p_codes[ch][:, k_cols].bitcast(FP8X4),
+                        lhsT_scale=p_scales[ch][:, k_cols],
+                        rhs=xn_codes[ch][:, d_cols].bitcast(FP8X4),
+                        rhs_scale=xn_scales[ch][:, d_cols],
+                        start=(c == 0),
+                        stop=(c == CHUNKS_PER_BATCH - 1),
+                    )
+                nc.vector.scalar_tensor_tensor(
+                    out=v[b, kc][:, d_cols],
+                    in0=c2T[:, kc, d_cols],
+                    scalar=neg_a_sum[:, b, kc : kc + 1],
+                    in1=acc[:],
+                    op0=ALU.mult,
+                    op1=ALU.add,
+                )
+
+        def square_sum(b, kc):
+            if kc == 0:
+                sum_vv[b] = stage2.tile([P, KC], F32, tag="sum_vv", name="sum_vv", bufs=3)
+            squares = scrap.tile([P, D], BF16, tag="squares")
+            nc.scalar.activation(out=squares[:], in_=v[b, kc][:], func=ACT.Square, accum_out=sum_vv[b][:, kc : kc + 1])
+
+        def factor_part(b, part):
+            if part == 0:
+                inv_norm[b] = stage2.tile([P, KC], F32, tag="inv_norm", name="inv_norm", bufs=3)
+                nc.vector.tensor_scalar(
+                    out=inv_norm[b][:], in0=sum_vv[b][:], scalar1=NORM_EPS * NORM_EPS, scalar2=None, op0=ALU.max
+                )
+                nc.gpsimd.tensor_tensor(out=inv_norm[b][:], in0=inv_norm[b][:], in1=neg_half[:], op=ALU.pow)
+            if part == 1:
+                unit = stage2.tile([P, KC], F32, tag="unit")
+                unit_sum[b] = stage2.tile([P, 1], F32, tag="unit_sum", name="unit_sum")
+                nc.vector.tensor_tensor(out=unit[:], in0=sum_vv[b][:], in1=inv_norm[b][:], op=ALU.mult)
+                nc.vector.tensor_tensor(out=unit[:], in0=unit[:], in1=inv_norm[b][:], op=ALU.mult)
+                nc.vector.tensor_reduce(out=unit_sum[b][:], in_=unit[:], axis=AXIS_X, op=ALU.add)
+            if part == 2:
+                inv_total[b] = stage2.tile([P, 1], F32, tag="inv_total", name="inv_total")
+                nc.vector.tensor_scalar(
+                    out=inv_total[b][:],
+                    in0=small[:, TOTALS + b : TOTALS + b + 1],
+                    scalar1=NORM_EPS * NORM_EPS,
+                    scalar2=None,
+                    op0=ALU.max,
+                )
+                nc.gpsimd.tensor_tensor(out=inv_total[b][:], in0=inv_total[b][:], in1=neg_half[:, 0:1], op=ALU.pow)
+            if part == 3:
+                factor[b] = stage2.tile([P, KC], F32, tag="factor", name="factor", bufs=3)
+                nc.vector.tensor_scalar(
+                    out=factor[b][:], in0=inv_norm[b][:], scalar1=inv_total[b][:, 0:1], scalar2=None, op0=ALU.mult
+                )
+
+        def add_over_partitions(b):
+            nc.tensor.matmul(
+                out=small[:, TOTALS + b : TOTALS + b + 1], lhsT=ones_f[:], rhs=unit_sum[b][:], start=True, stop=True
+            )
+
+        def scale_v(b, kc):
+            nc.vector.tensor_scalar(
+                out=v[b, kc][:], in0=v[b, kc][:], scalar1=factor[b][:, kc : kc + 1], scalar2=None, op0=ALU.mult
+            )
+
+        def transpose_and_store(b, kc):
+            for dg in range(2):
+                if kc == 0:
+                    out_rows[b, dg] = stage2.tile([P, HALF_TILES, K], F32, tag="out_rows", name="out_rows", bufs=4)
+                vt = transpose_bank([P, HALF_TILES, P], F32)
+                for t in range(HALF_TILES):
+                    first = (dg * HALF_TILES + t) * P
+                    nc.tensor.transpose(vt[:, t, :], v[b, kc][:, first : first + P], ident_f[:])
+                copy_out(dg == 1 and kc % 2 == 1, out_rows[b, dg][:, :, kc * P : (kc + 1) * P], vt[:])
+            if kc == KC - 1:
+                dram_rows = out[b].rearrange("(dg t q k) -> dg q t k", dg=2, q=P, k=K)
+                for dg in range(2):
+                    nc.sync.dma_start(out=dram_rows[dg], in_=out_rows[b, dg][:])
+
+        STEPS = B * KC
+        LAG = 2 * KC
+        for step in range(STEPS + LAG):
+            if step < STEPS:
+                second_matmul(step // KC, step % KC)
+            since_batch_end = step % KC
+            done_batch = step // KC - 1
+            if 0 <= done_batch < B and since_batch_end == 2:
+                add_over_partitions(done_batch)
+            if step >= LAG:
+                transpose_and_store((step - LAG) // KC, (step - LAG) % KC)
+            if step < STEPS:
+                square_sum(step // KC, step % KC)
+            if 0 <= done_batch < B:
+                factor_part(done_batch, since_batch_end)
+            ahead = step + 1 - LAG
+            if 0 <= ahead < STEPS:
+                scale_v(ahead // KC, ahead % KC)

@@ -33,7 +33,6 @@ FLOPS = 2 * ROWS * D * K * 2
 def tile_modelnew_t_kernel(tc, x, clusters, clusters2, bn_gamma, bn_beta, out):
     nc = tc.nc
     with ExitStack() as ctx:
-        ctx.enter_context(tc.manual_schedule())
         keep = ctx.enter_context(tc.tile_pool(name="keep", bufs=1))
         wide = ctx.enter_context(tc.tile_pool(name="wide", bufs=2 * CHUNKS))
         scrap = ctx.enter_context(tc.tile_pool(name="scrap", bufs=2))
@@ -77,7 +76,7 @@ def tile_modelnew_t_kernel(tc, x, clusters, clusters2, bn_gamma, bn_beta, out):
         bn_shift = keep.tile([P, KC], F32)
         neg_a_sum = keep.tile([P, B, KC], F32)
         small = psum.tile([P, BANK], F32, tag="small")
-        TOTALS = B * KC
+        TOTALS = 0
 
         a_sb = {}
 
@@ -239,16 +238,16 @@ def tile_modelnew_t_kernel(tc, x, clusters, clusters2, bn_gamma, bn_beta, out):
         p_codes = {}
         p_scales = {}
         a_sum_ps = {}
-        a_sum_sb = {}
 
         def normalise(ch):
             for kc in range(KC):
-                nc.scalar.activation(
+                nc.vector.tensor_scalar(
                     out=a_view(ch, kc),
-                    in_=a_view(ch, kc),
-                    func=ACT.Identity,
-                    scale=bn_scale[:, kc : kc + 1],
-                    bias=bn_shift[:, kc : kc + 1],
+                    in0=a_view(ch, kc),
+                    scalar1=bn_scale[:, kc : kc + 1],
+                    scalar2=bn_shift[:, kc : kc + 1],
+                    op0=ALU.mult,
+                    op1=ALU.add,
                 )
 
         def transpose_z(ch):
@@ -260,7 +259,7 @@ def tile_modelnew_t_kernel(tc, x, clusters, clusters2, bn_gamma, bn_beta, out):
                     )
 
         def exponentials(ch):
-            e[ch] = stage2.tile([P, PACK, K], F32, tag="e", name="e")
+            e[ch] = stage2.tile([P, PACK, K], F32, tag="e", name="e", bufs=3)
             neg_max[ch] = stage2.tile([P, PACK], F32, tag="neg_max", name="neg_max")
             row_sum[ch] = stage2.tile([P, PACK], F32, tag="row_sum", name="row_sum")
             for j in range(PACK):
@@ -276,46 +275,39 @@ def tile_modelnew_t_kernel(tc, x, clusters, clusters2, bn_gamma, bn_beta, out):
                     accum_out=row_sum[ch][:, j : j + 1],
                 )
 
+        def divide(ch):
+            for j in range(PACK):
+                nc.scalar.activation(
+                    out=e[ch][:, j, :], in_=e[ch][:, j, :], func=ACT.Copy, scale=recip[ch][:, j : j + 1]
+                )
+
         def sum_p(ch):
             b, c = divmod(ch, CHUNKS_PER_BATCH)
             if c == 0:
                 a_sum_ps[b] = sum_bank()
             for j in range(PACK):
-                nc.tensor.matmul(
-                    out=a_sum_ps[b][:],
-                    lhsT=recip[ch][:, j : j + 1].to_broadcast([P, P]),
-                    rhs=e[ch][:, j, :],
-                    start=(c == 0 and j == 0),
-                    stop=(c == CHUNKS_PER_BATCH - 1 and j == PACK - 1),
-                )
-
-        def copy_a_sum(b):
-            a_sum_sb[b] = stage2.tile([P, K], F32, tag="a_sum_sb", name="a_sum_sb")
-            nc.scalar.copy(out=a_sum_sb[b][:], in_=a_sum_ps[b][:])
-
-        def turn_a_sum(b):
-            for kc in range(KC):
-                nc.tensor.matmul(
-                    out=small[:, b * KC + kc : b * KC + kc + 1],
-                    lhsT=a_sum_sb[b][:, kc * P : (kc + 1) * P],
-                    rhs=ident_f[:, 0:1],
-                    start=True,
-                    stop=True,
-                )
+                for kc in range(KC):
+                    nc.tensor.matmul(
+                        out=a_sum_ps[b][:, kc * P : (kc + 1) * P],
+                        lhsT=e[ch][:, j, kc * P : (kc + 1) * P],
+                        rhs=ident_f[:],
+                        is_transpose=True,
+                        start=(c == 0 and j == 0 and kc == 0),
+                        stop=(c == CHUNKS_PER_BATCH - 1 and j == PACK - 1 and kc == KC - 1),
+                    )
 
         def negate_a_sum(b):
-            nc.vector.tensor_scalar(
-                out=neg_a_sum[:, b, :], in0=small[:, b * KC : (b + 1) * KC], scalar1=-1.0, scalar2=None, op0=ALU.mult
+            nc.vector.tensor_reduce(
+                out=neg_a_sum[:, b, :],
+                in_=a_sum_ps[b][:].rearrange("k (kc n) -> k kc n", kc=KC),
+                axis=AXIS_X,
+                op=ALU.add,
+                negate=True,
             )
 
         def round_p(ch):
             p_grouped[ch] = stage2.tile([P, K, PACK], BF16, tag="p_grouped", name="p_grouped", align_bytes=64)
-            nc.vector.tensor_tensor(
-                out=p_grouped[ch][:],
-                in0=e[ch][:].rearrange("q j k -> q k j"),
-                in1=recip[ch][:].unsqueeze(1).to_broadcast([P, K, PACK]),
-                op=ALU.mult,
-            )
+            nc.vector.tensor_copy(out=p_grouped[ch][:], in_=e[ch][:].rearrange("q j k -> q k j"))
 
         def quantise_p(ch):
             p_codes[ch] = stage2.tile([P, K], U32, tag="p_codes", name="p_codes", bufs=CHUNKS, align_bytes=64)
@@ -332,24 +324,19 @@ def tile_modelnew_t_kernel(tc, x, clusters, clusters2, bn_gamma, bn_beta, out):
         for ch in range(CHUNKS):
             summed = ch // CHUNKS_PER_BATCH - 1 if ch % CHUNKS_PER_BATCH == 0 else -1
             exponentials(ch)
-            if summed >= 0:
-                copy_a_sum(summed)
             if ch > 0:
                 quantise_p(ch - 1)
             recip[ch] = stage2.tile([P, PACK], F32, tag="recip", name="recip")
             nc.vector.reciprocal(out=recip[ch][:], in_=row_sum[ch][:])
+            divide(ch)
             if ch + 1 < CHUNKS:
                 transpose_z(ch + 1)
-            if summed >= 0:
-                turn_a_sum(summed)
             sum_p(ch)
             round_p(ch)
             if summed >= 0:
                 negate_a_sum(summed)
             if ch + 2 < CHUNKS:
                 normalise(ch + 2)
-        copy_a_sum(B - 1)
-        turn_a_sum(B - 1)
         quantise_p(CHUNKS - 1)
         negate_a_sum(B - 1)
 

@@ -33,6 +33,7 @@ FLOPS = 2 * ROWS * D * K * 2
 def tile_modelnew_t_kernel(tc, x, clusters, clusters2, bn_gamma, bn_beta, out):
     nc = tc.nc
     with ExitStack() as ctx:
+        ctx.enter_context(tc.manual_schedule())
         keep = ctx.enter_context(tc.tile_pool(name="keep", bufs=1))
         wide = ctx.enter_context(tc.tile_pool(name="wide", bufs=2 * CHUNKS))
         scrap = ctx.enter_context(tc.tile_pool(name="scrap", bufs=2))
@@ -321,24 +322,25 @@ def tile_modelnew_t_kernel(tc, x, clusters, clusters2, bn_gamma, bn_beta, out):
         normalise(0)
         normalise(1)
         transpose_z(0)
-        for ch in range(CHUNKS):
-            summed = ch // CHUNKS_PER_BATCH - 1 if ch % CHUNKS_PER_BATCH == 0 else -1
-            exponentials(ch)
+        for ch in range(CHUNKS + 1):
+            if ch < CHUNKS:
+                exponentials(ch)
             if ch > 0:
-                quantise_p(ch - 1)
-            recip[ch] = stage2.tile([P, PACK], F32, tag="recip", name="recip")
-            nc.vector.reciprocal(out=recip[ch][:], in_=row_sum[ch][:])
-            divide(ch)
+                round_p(ch - 1)
+            if ch < CHUNKS:
+                recip[ch] = stage2.tile([P, PACK], F32, tag="recip", name="recip", bufs=3)
+                nc.vector.reciprocal(out=recip[ch][:], in_=row_sum[ch][:])
+                divide(ch)
             if ch + 1 < CHUNKS:
                 transpose_z(ch + 1)
-            sum_p(ch)
-            round_p(ch)
-            if summed >= 0:
-                negate_a_sum(summed)
+            if ch < CHUNKS:
+                sum_p(ch)
             if ch + 2 < CHUNKS:
                 normalise(ch + 2)
-        quantise_p(CHUNKS - 1)
-        negate_a_sum(B - 1)
+            if ch > 0:
+                quantise_p(ch - 1)
+            if ch > 0 and ch % CHUNKS_PER_BATCH == 0:
+                negate_a_sum(ch // CHUNKS_PER_BATCH - 1)
 
         v = {}
         sum_vv = {}

@@ -23,6 +23,7 @@ CHUNKS_PER_BATCH = N // CHUNK
 D_PASSES = D // K_PASS
 KC = K // P
 D_TILES = D // P
+EARLY = 2
 BANK = 512
 BN_EPS = 1e-5
 NORM_EPS = 1e-12
@@ -76,8 +77,6 @@ def tile_modelnew_t_kernel(tc, x, clusters, clusters2, bn_gamma, bn_beta, out):
         bn_scale = keep.tile([P, KC], F32)
         bn_shift = keep.tile([P, KC], F32)
         neg_a_sum = keep.tile([P, B, KC], F32)
-        small = psum.tile([P, BANK], F32, tag="small")
-        TOTALS = 0
 
         a_sb = {}
 
@@ -285,7 +284,7 @@ def tile_modelnew_t_kernel(tc, x, clusters, clusters2, bn_gamma, bn_beta, out):
         def sum_p(ch):
             b, c = divmod(ch, CHUNKS_PER_BATCH)
             if c == 0:
-                a_sum_ps[b] = sum_bank()
+                a_sum_ps[b] = psum.tile([P, BANK], F32, tag="small", name="a_sum")
             for j in range(PACK):
                 for kc in range(KC):
                     nc.tensor.matmul(
@@ -319,34 +318,11 @@ def tile_modelnew_t_kernel(tc, x, clusters, clusters2, bn_gamma, bn_beta, out):
                 in_=p_grouped[ch][:].rearrange("q k j -> q (k j)"),
             )
 
-        normalise(0)
-        normalise(1)
-        transpose_z(0)
-        for ch in range(CHUNKS + 1):
-            if ch < CHUNKS:
-                exponentials(ch)
-            if ch > 0:
-                round_p(ch - 1)
-            if ch < CHUNKS:
-                recip[ch] = stage2.tile([P, PACK], F32, tag="recip", name="recip", bufs=3)
-                nc.vector.reciprocal(out=recip[ch][:], in_=row_sum[ch][:])
-                divide(ch)
-            if ch + 1 < CHUNKS:
-                transpose_z(ch + 1)
-            if ch < CHUNKS:
-                sum_p(ch)
-            if ch + 2 < CHUNKS:
-                normalise(ch + 2)
-            if ch > 0:
-                quantise_p(ch - 1)
-            if ch > 0 and ch % CHUNKS_PER_BATCH == 0:
-                negate_a_sum(ch // CHUNKS_PER_BATCH - 1)
-
         v = {}
         sum_vv = {}
-        inv_norm = {}
+        floored = {}
         unit_sum = {}
-        inv_total = {}
+        total_ps = {}
         factor = {}
         out_rows = {}
         HALF_TILES = D_TILES // 2
@@ -379,78 +355,131 @@ def tile_modelnew_t_kernel(tc, x, clusters, clusters2, bn_gamma, bn_beta, out):
 
         def square_sum(b, kc):
             if kc == 0:
-                sum_vv[b] = stage2.tile([P, KC], F32, tag="sum_vv", name="sum_vv", bufs=3)
+                sum_vv[b] = stage2.tile([P, KC], F32, tag="sum_vv", name="sum_vv")
             squares = scrap.tile([P, D], BF16, tag="squares")
             nc.scalar.activation(out=squares[:], in_=v[b, kc][:], func=ACT.Square, accum_out=sum_vv[b][:, kc : kc + 1])
 
-        def factor_part(b, part):
-            if part == 0:
-                inv_norm[b] = stage2.tile([P, KC], F32, tag="inv_norm", name="inv_norm", bufs=3)
-                nc.vector.tensor_scalar(
-                    out=inv_norm[b][:], in0=sum_vv[b][:], scalar1=NORM_EPS * NORM_EPS, scalar2=None, op0=ALU.max
-                )
-                nc.gpsimd.tensor_tensor(out=inv_norm[b][:], in0=inv_norm[b][:], in1=neg_half[:], op=ALU.pow)
-            if part == 1:
-                unit = stage2.tile([P, KC], F32, tag="unit")
-                unit_sum[b] = stage2.tile([P, 1], F32, tag="unit_sum", name="unit_sum")
-                nc.vector.tensor_tensor(out=unit[:], in0=sum_vv[b][:], in1=inv_norm[b][:], op=ALU.mult)
-                nc.vector.tensor_tensor(out=unit[:], in0=unit[:], in1=inv_norm[b][:], op=ALU.mult)
-                nc.vector.tensor_reduce(out=unit_sum[b][:], in_=unit[:], axis=AXIS_X, op=ALU.add)
-            if part == 2:
-                inv_total[b] = stage2.tile([P, 1], F32, tag="inv_total", name="inv_total")
-                nc.vector.tensor_scalar(
-                    out=inv_total[b][:],
-                    in0=small[:, TOTALS + b : TOTALS + b + 1],
-                    scalar1=NORM_EPS * NORM_EPS,
-                    scalar2=None,
-                    op0=ALU.max,
-                )
-                nc.gpsimd.tensor_tensor(out=inv_total[b][:], in0=inv_total[b][:], in1=neg_half[:, 0:1], op=ALU.pow)
-            if part == 3:
-                factor[b] = stage2.tile([P, KC], F32, tag="factor", name="factor", bufs=3)
-                nc.vector.tensor_scalar(
-                    out=factor[b][:], in0=inv_norm[b][:], scalar1=inv_total[b][:, 0:1], scalar2=None, op0=ALU.mult
-                )
+        def unit_norms(b):
+            floored[b] = stage2.tile([P, KC], F32, tag="floored", name="floored")
+            unit = stage2.tile([P, KC], F32, tag="unit")
+            unit_sum[b] = stage2.tile([P, 1], F32, tag="unit_sum", name="unit_sum")
+            nc.vector.tensor_scalar(
+                out=floored[b][:], in0=sum_vv[b][:], scalar1=NORM_EPS * NORM_EPS, scalar2=None, op0=ALU.max
+            )
+            nc.vector.reciprocal(out=unit[:], in_=floored[b][:])
+            nc.vector.tensor_tensor(out=unit[:], in0=unit[:], in1=sum_vv[b][:], op=ALU.mult)
+            nc.vector.tensor_reduce(out=unit_sum[b][:], in_=unit[:], axis=AXIS_X, op=ALU.add)
 
         def add_over_partitions(b):
-            nc.tensor.matmul(
-                out=small[:, TOTALS + b : TOTALS + b + 1], lhsT=ones_f[:], rhs=unit_sum[b][:], start=True, stop=True
+            total_ps[b] = psum.tile([P, 1], F32, tag="small", name="total")
+            nc.tensor.matmul(out=total_ps[b][:], lhsT=ones_f[:], rhs=unit_sum[b][:], start=True, stop=True)
+
+        def make_factor(b):
+            factor[b] = stage2.tile([P, KC], F32, tag="factor", name="factor")
+            nc.vector.scalar_tensor_tensor(
+                out=factor[b][:],
+                in0=total_ps[b][:].to_broadcast([P, KC]),
+                scalar=NORM_EPS * NORM_EPS,
+                in1=floored[b][:],
+                op0=ALU.max,
+                op1=ALU.mult,
+            )
+            nc.gpsimd.tensor_tensor(out=factor[b][:], in0=factor[b][:], in1=neg_half[:], op=ALU.pow)
+
+        def scale_v(b, kc, engine):
+            engine.tensor_scalar(
+                out=v[b, kc][:],
+                in0=v[b, kc][:],
+                scalar1=factor[b][:, kc : kc + 1],
+                scalar2=0.0,
+                op0=ALU.mult,
+                op1=ALU.add,
             )
 
-        def scale_v(b, kc):
-            nc.vector.tensor_scalar(
-                out=v[b, kc][:], in0=v[b, kc][:], scalar1=factor[b][:, kc : kc + 1], scalar2=None, op0=ALU.mult
-            )
+        def dram_tiles(b):
+            return out[b].rearrange("(t q k) -> q t k", q=P, k=K)
 
-        def transpose_and_store(b, kc):
-            for dg in range(2):
-                if kc == 0:
-                    out_rows[b, dg] = stage2.tile([P, HALF_TILES, K], F32, tag="out_rows", name="out_rows", bufs=4)
-                vt = transpose_bank([P, HALF_TILES, P], F32)
-                for t in range(HALF_TILES):
-                    first = (dg * HALF_TILES + t) * P
-                    nc.tensor.transpose(vt[:, t, :], v[b, kc][:, first : first + P], ident_f[:])
-                copy_out(dg == 1 and kc % 2 == 1, out_rows[b, dg][:, :, kc * P : (kc + 1) * P], vt[:])
+        def transpose_group(b, dg, kc, on_vector):
+            if kc == 0:
+                out_rows[b, dg] = stage2.tile([P, HALF_TILES, K], F32, tag="out_rows", name="out_rows", bufs=4)
+            vt = transpose_bank([P, HALF_TILES, P], F32)
+            for t in range(HALF_TILES):
+                first = (dg * HALF_TILES + t) * P
+                nc.tensor.transpose(vt[:, t, :], v[b, kc][:, first : first + P], ident_f[:])
+            copy_out(on_vector, out_rows[b, dg][:, :, kc * P : (kc + 1) * P], vt[:])
             if kc == KC - 1:
-                dram_rows = out[b].rearrange("(dg t q k) -> dg q t k", dg=2, q=P, k=K)
-                for dg in range(2):
-                    nc.sync.dma_start(out=dram_rows[dg], in_=out_rows[b, dg][:])
+                tiles = slice(dg * HALF_TILES, (dg + 1) * HALF_TILES)
+                nc.sync.dma_start(out=dram_tiles(b)[:, tiles, :], in_=out_rows[b, dg][:])
 
-        STEPS = B * KC
-        LAG = 2 * KC
-        for step in range(STEPS + LAG):
-            if step < STEPS:
-                second_matmul(step // KC, step % KC)
-            since_batch_end = step % KC
-            done_batch = step // KC - 1
-            if 0 <= done_batch < B and since_batch_end == 2:
-                add_over_partitions(done_batch)
-            if step >= LAG:
-                transpose_and_store((step - LAG) // KC, (step - LAG) % KC)
-            if step < STEPS:
-                square_sum(step // KC, step % KC)
-            if 0 <= done_batch < B:
-                factor_part(done_batch, since_batch_end)
-            ahead = step + 1 - LAG
-            if 0 <= ahead < STEPS:
-                scale_v(ahead // KC, ahead % KC)
+        def transpose_tile(b, t, on_vector):
+            dg, tt = divmod(t, HALF_TILES)
+            if tt == 0:
+                out_rows[b, dg] = stage2.tile([P, HALF_TILES, K], F32, tag="out_rows", name="out_rows", bufs=4)
+            vt = transpose_bank([P, K], F32)
+            for kc in range(KC):
+                nc.tensor.transpose(vt[:, kc * P : (kc + 1) * P], v[b, kc][:, t * P : (t + 1) * P], ident_f[:])
+            copy_out(on_vector, out_rows[b, dg][:, tt, :], vt[:])
+            nc.sync.dma_start(out=dram_tiles(b)[:, t, :], in_=out_rows[b, dg][:, tt, :])
+
+        normalise(0)
+        normalise(1)
+        transpose_z(0)
+        for ch in range(CHUNKS + 1):
+            if ch < CHUNKS:
+                exponentials(ch)
+            if ch > 0:
+                round_p(ch - 1)
+            if ch < CHUNKS:
+                recip[ch] = stage2.tile([P, PACK], F32, tag="recip", name="recip", bufs=3)
+                nc.vector.reciprocal(out=recip[ch][:], in_=row_sum[ch][:])
+                divide(ch)
+            if ch + 1 < CHUNKS:
+                transpose_z(ch + 1)
+            if ch > 0 and ch % CHUNKS_PER_BATCH == 0:
+                negate_a_sum(ch // CHUNKS_PER_BATCH - 1)
+            if ch == CHUNKS - 1:
+                for kc in range(EARLY):
+                    second_matmul(0, kc)
+            if ch < CHUNKS:
+                sum_p(ch)
+            if ch + 2 < CHUNKS:
+                normalise(ch + 2)
+            if ch > 0:
+                quantise_p(ch - 1)
+            if ch == CHUNKS - 1:
+                for kc in range(EARLY):
+                    square_sum(0, kc)
+
+        OUT_LAG = 2 * KC - 1
+        for step in range(EARLY, B * KC):
+            b, kc = divmod(step, KC)
+            second_matmul(b, kc)
+            if b > 0 and kc == 1:
+                add_over_partitions(b - 1)
+            if step >= OUT_LAG:
+                out_b, out_kc = divmod(step - OUT_LAG, KC)
+                transpose_group(out_b, 0, out_kc, True)
+                transpose_group(out_b, 1, out_kc, False)
+            square_sum(b, kc)
+            if b > 0 and kc == 0:
+                unit_norms(b - 1)
+            if b > 0 and kc == 1:
+                make_factor(b - 1)
+                for scaled in range(KC):
+                    scale_v(b - 1, scaled, nc.gpsimd)
+        before, last = B - 2, B - 1
+        transpose_group(before, 0, 1, True)
+        transpose_group(before, 1, 1, False)
+        unit_norms(last)
+        transpose_group(before, 0, 2, True)
+        add_over_partitions(last)
+        transpose_group(before, 1, 2, False)
+        make_factor(last)
+        transpose_group(before, 0, 3, False)
+        transpose_group(before, 1, 3, True)
+        scale_v(last, 0, nc.vector)
+        scale_v(last, 1, nc.vector)
+        scale_v(last, 2, nc.vector)
+        scale_v(last, 3, nc.vector)
+        for t in range(D_TILES):
+            transpose_tile(last, t, t % 2 == 0)

@@ -24,6 +24,9 @@ D_PASSES = D // K_PASS
 KC = K // P
 D_TILES = D // P
 EARLY = 2
+NV = (0, 1, 2)
+V_STATS = ((7, 1), (7, 3))
+V_XCP = [(ch, j) for ch in range(1, 8) for j in ((1, 3) if ch < 6 else (0, 1, 3))]
 BANK = 512
 BN_EPS = 1e-5
 NORM_EPS = 1e-12
@@ -83,19 +86,61 @@ def tile_modelnew_t_kernel(tc, x, clusters, clusters2, bn_gamma, bn_beta, out):
         def a_view(ch, kc):
             return a_sb[ch, kc // 2][:, kc % 2, :]
 
+        def normalise_group(ch, kc, on_vector):
+            if on_vector:
+                nc.vector.tensor_scalar(
+                    out=a_view(ch, kc),
+                    in0=a_view(ch, kc),
+                    scalar1=bn_scale[:, kc : kc + 1],
+                    scalar2=bn_shift[:, kc : kc + 1],
+                    op0=ALU.mult,
+                    op1=ALU.add,
+                )
+            else:
+                nc.scalar.activation(
+                    out=a_view(ch, kc),
+                    in_=a_view(ch, kc),
+                    func=ACT.Identity,
+                    scale=bn_scale[:, kc : kc + 1],
+                    bias=bn_shift[:, kc : kc + 1],
+                )
+
+        def normalise(ch, on_vector):
+            for kc in range(KC):
+                normalise_group(ch, kc, kc in on_vector)
+
+        def normalise_scalar(ch):
+            for kc in range(KC):
+                if kc not in NV:
+                    normalise_group(ch, kc, False)
+
+        def normalise_vector(ch):
+            for kc in NV:
+                normalise_group(ch, kc, True)
+
+        xn_grouped = {}
+
+        def quantise_xn(ch):
+            nc.vector.quantize_mx(
+                out=xn_codes[ch][:].bitcast(FP8X4), scales=xn_scales[ch][:], in_=xn_grouped[ch][:]
+            )
+
         with tc.tile_pool(name="stage1", bufs=2) as stage1:
             x_tiles = {}
             xd_grouped = {}
             xd_codes = {}
             xd_scales = {}
-            xn_grouped = {}
             X_BUFS = 4
 
-            def load_chunk(ch):
+            def load_chunk(ch, pieces=1):
                 b, c = divmod(ch, CHUNKS_PER_BATCH)
                 x_tiles[ch] = stage1.tile([P, PACK * D], BF16, tag="x_sb", name="x_sb", bufs=X_BUFS)
-                rows = x[b, c * CHUNK : (c + 1) * CHUNK, :]
-                nc.sync.dma_start(out=x_tiles[ch][:], in_=rows.rearrange("(q j) d -> q (j d)", j=PACK))
+                rows = x[b, c * CHUNK : (c + 1) * CHUNK, :].rearrange("(q j) d -> q (j d)", j=PACK)
+                span = PACK * D // pieces
+                for first in range(0, PACK * D, span):
+                    nc.sync.dma_start(
+                        out=x_tiles[ch][:, first : first + span], in_=rows[:, first : first + span]
+                    )
 
             def transpose_chunk(ch):
                 x_words = x_tiles[ch][:].bitcast(F32)
@@ -109,7 +154,7 @@ def tile_modelnew_t_kernel(tc, x, clusters, clusters2, bn_gamma, bn_beta, out):
                         first = j * (D // 2) + h * P
                         nc.tensor.transpose(xt[:, h * P : (h + 1) * P], x_words[:, first : first + P], ident_f[:])
                     copy_out(
-                        j % 2 == 1,
+                        (ch, j) in V_XCP,
                         xd_words[:, :, j * P : (j + 1) * P, :],
                         xt[:].rearrange("q (g u n) -> q g n u", g=D_PASSES, u=2),
                     )
@@ -142,31 +187,52 @@ def tile_modelnew_t_kernel(tc, x, clusters, clusters2, bn_gamma, bn_beta, out):
                             start=(g == 0),
                             stop=(g == D_PASSES - 1),
                         )
-                    nc.scalar.activation(
-                        out=a_view(ch, kc), in_=acc[:], func=ACT.Identity, accum_out=sum_a[:, kc, ch : ch + 1]
-                    )
                     squares = scrap.tile([P, D], BF16, tag="squares")
-                    nc.scalar.activation(
-                        out=squares[:, 0:CHUNK], in_=acc[:], func=ACT.Square, accum_out=sum_aa[:, kc, ch : ch + 1]
+                    if (ch, kc) in V_STATS:
+                        nc.vector.tensor_scalar(
+                            out=a_view(ch, kc),
+                            in0=acc[:],
+                            scalar1=1.0,
+                            scalar2=None,
+                            op0=ALU.mult,
+                            op1=ALU.add,
+                            accum_out=sum_a[:, kc, ch : ch + 1],
+                        )
+                        nc.vector.scalar_tensor_tensor(
+                            out=squares[:, 0:CHUNK],
+                            in0=acc[:],
+                            scalar=1.0,
+                            in1=a_view(ch, kc),
+                            op0=ALU.mult,
+                            op1=ALU.mult,
+                            accum_out=sum_aa[:, kc, ch : ch + 1],
+                        )
+                    else:
+                        nc.scalar.activation(
+                            out=a_view(ch, kc), in_=acc[:], func=ACT.Identity, accum_out=sum_a[:, kc, ch : ch + 1]
+                        )
+                        nc.scalar.activation(
+                            out=squares[:, 0:CHUNK], in_=acc[:], func=ACT.Square, accum_out=sum_aa[:, kc, ch : ch + 1]
+                        )
+
+            def regroup_xn(ch, parts):
+                if parts.start == 0:
+                    xn_grouped[ch] = scrap.tile(
+                        [P, D * PACK], BF16, tag="xn_grouped", name="xn_grouped", align_bytes=64
                     )
-
-            def regroup_xn(ch):
-                xn_grouped[ch] = stage1.tile([P, D * PACK], BF16, tag="xn_grouped", name="xn_grouped", align_bytes=64)
+                s = slice(parts.start * D // 16, parts.stop * D // 16)
                 nc.vector.tensor_copy(
-                    out=xn_grouped[ch][:].rearrange("q (s i j) -> q s j i", i=4, j=PACK),
-                    in_=x_tiles[ch][:].rearrange("q (j s i) -> q s j i", j=PACK, i=4),
+                    out=xn_grouped[ch][:].rearrange("q (s i j) -> q s j i", i=4, j=PACK)[:, s],
+                    in_=x_tiles[ch][:].rearrange("q (j s i) -> q s j i", j=PACK, i=4)[:, s],
                 )
 
-            def quantise_xn(ch):
-                nc.vector.quantize_mx(
-                    out=xn_codes[ch][:].bitcast(FP8X4), scales=xn_scales[ch][:], in_=xn_grouped[ch][:]
-                )
-
-            load_chunk(0)
             c_raw = stage1.tile([P, 2 * D_PASSES, 2, K], BF16, bufs=1)
-            nc.sync.dma_start(
-                out=c_raw[:], in_=clusters.rearrange("(h q e) k -> q h e k", h=2 * D_PASSES, e=2)
-            )
+            load_chunk(0, 2)
+            for g in range(D_PASSES):
+                nc.sync.dma_start(
+                    out=c_raw[:, 2 * g : 2 * g + 2],
+                    in_=clusters[g * K_PASS : (g + 1) * K_PASS].rearrange("(u q e) k -> q u e k", u=2, e=2),
+                )
             for ch in range(1, X_BUFS):
                 load_chunk(ch)
             gb_rows = stage1.tile([P, P], BF16, bufs=1)
@@ -174,30 +240,38 @@ def tile_modelnew_t_kernel(tc, x, clusters, clusters2, bn_gamma, bn_beta, out):
             nc.sync.dma_start(out=gb_rows[0:KC, :], in_=bn_gamma.rearrange("(r k) -> r k", k=P))
             nc.sync.dma_start(out=gb_rows[KC : 2 * KC, :], in_=bn_beta.rearrange("(r k) -> r k", k=P))
 
-            transpose_chunk(0)
             c_grouped = stage1.tile([P, D_PASSES, K, PACK], BF16, bufs=1, align_bytes=64)
-            for g in range(D_PASSES):
+            c_codes = stage1.tile([P, D_PASSES * K], U32, bufs=1, align_bytes=64)
+            c_scales = stage1.tile([P, D_PASSES * K], U8, bufs=1, align_bytes=64)
+
+            def group_clusters(g):
                 nc.vector.tensor_copy(
                     out=c_grouped[:, g].rearrange("q k (u e) -> q k u e", e=2),
                     in_=c_raw[:, 2 * g : 2 * g + 2].rearrange("q u e k -> q k u e"),
                 )
+
+            def quantise_clusters(g):
+                nc.vector.quantize_mx(
+                    out=c_codes[:, g * K : (g + 1) * K].bitcast(FP8X4),
+                    scales=c_scales[:, g * K : (g + 1) * K],
+                    in_=c_grouped[:, g].rearrange("q k t -> q (k t)"),
+                )
+
+            transpose_chunk(0)
+            group_clusters(0)
+            group_clusters(1)
+            quantise_clusters(0)
             quantise_xd(0)
-            c_codes = stage1.tile([P, D_PASSES * K], U32, bufs=1, align_bytes=64)
-            c_scales = stage1.tile([P, D_PASSES * K], U8, bufs=1, align_bytes=64)
-            nc.vector.quantize_mx(
-                out=c_codes[:].bitcast(FP8X4),
-                scales=c_scales[:],
-                in_=c_grouped[:].rearrange("q g k t -> q (g k t)"),
-            )
+            quantise_clusters(1)
 
             for ch in range(CHUNKS):
                 if ch + 1 < CHUNKS:
                     transpose_chunk(ch + 1)
                 first_matmul(ch)
-                regroup_xn(ch)
                 if ch + 1 < CHUNKS:
+                    regroup_xn(ch, range(0, 4))
                     quantise_xd(ch + 1)
-                quantise_xn(ch)
+                    quantise_xn(ch)
                 if ch + X_BUFS < CHUNKS:
                     load_chunk(ch + X_BUFS)
 
@@ -215,18 +289,22 @@ def tile_modelnew_t_kernel(tc, x, clusters, clusters2, bn_gamma, bn_beta, out):
                     )
                 nc.scalar.copy(out=c2T[:, kc, :], in_=c2_ps[:])
 
-        nc.vector.tensor_reduce(out=mean[:], in_=sum_a[:], axis=AXIS_X, op=ALU.add)
-        nc.vector.tensor_reduce(out=mean_aa[:], in_=sum_aa[:], axis=AXIS_X, op=ALU.add)
-        nc.vector.tensor_scalar(out=mean[:], in0=mean[:], scalar1=1.0 / ROWS, scalar2=None, op0=ALU.mult)
-        nc.vector.tensor_tensor(out=var[:], in0=mean[:], in1=mean[:], op=ALU.mult)
-        nc.vector.scalar_tensor_tensor(
-            out=var[:], in0=mean_aa[:], scalar=1.0 / ROWS, in1=var[:], op0=ALU.mult, op1=ALU.subtract
-        )
-        nc.vector.tensor_scalar(out=var[:], in0=var[:], scalar1=0.0, scalar2=BN_EPS, op0=ALU.max, op1=ALU.add)
-        nc.gpsimd.tensor_tensor(out=rstd[:], in0=var[:], in1=neg_half[:], op=ALU.pow)
-        nc.vector.tensor_tensor(out=bn_scale[:], in0=gamma_beta[:, 0:KC], in1=rstd[:], op=ALU.mult)
-        nc.vector.tensor_tensor(out=bn_shift[:], in0=mean[:], in1=bn_scale[:], op=ALU.mult)
-        nc.vector.tensor_tensor(out=bn_shift[:], in0=gamma_beta[:, KC : 2 * KC], in1=bn_shift[:], op=ALU.subtract)
+            nc.vector.tensor_reduce(out=mean[:], in_=sum_a[:], axis=AXIS_X, op=ALU.add)
+            nc.vector.tensor_reduce(out=mean_aa[:], in_=sum_aa[:], axis=AXIS_X, op=ALU.add)
+            nc.vector.tensor_scalar(out=mean[:], in0=mean[:], scalar1=1.0 / ROWS, scalar2=None, op0=ALU.mult)
+            nc.vector.tensor_tensor(out=var[:], in0=mean[:], in1=mean[:], op=ALU.mult)
+            nc.vector.scalar_tensor_tensor(
+                out=var[:], in0=mean_aa[:], scalar=1.0 / ROWS, in1=var[:], op0=ALU.mult, op1=ALU.subtract
+            )
+            nc.vector.tensor_scalar(out=var[:], in0=var[:], scalar1=0.0, scalar2=BN_EPS, op0=ALU.max, op1=ALU.add)
+            nc.gpsimd.tensor_tensor(out=rstd[:], in0=var[:], in1=neg_half[:], op=ALU.pow)
+            regroup_xn(CHUNKS - 1, range(0, 2))
+            nc.vector.tensor_tensor(out=bn_scale[:], in0=gamma_beta[:, 0:KC], in1=rstd[:], op=ALU.mult)
+            nc.vector.tensor_tensor(out=bn_shift[:], in0=mean[:], in1=bn_scale[:], op=ALU.mult)
+            nc.vector.tensor_tensor(out=bn_shift[:], in0=gamma_beta[:, KC : 2 * KC], in1=bn_shift[:], op=ALU.subtract)
+
+            normalise(0, (1, 3))
+            regroup_xn(CHUNKS - 1, range(2, 4))
 
         stage2 = ctx.enter_context(tc.tile_pool(name="stage2", bufs=2, reuse_waits="tile"))
         zt = {}
@@ -239,17 +317,6 @@ def tile_modelnew_t_kernel(tc, x, clusters, clusters2, bn_gamma, bn_beta, out):
         p_scales = {}
         a_sum_ps = {}
 
-        def normalise(ch):
-            for kc in range(KC):
-                nc.vector.tensor_scalar(
-                    out=a_view(ch, kc),
-                    in0=a_view(ch, kc),
-                    scalar1=bn_scale[:, kc : kc + 1],
-                    scalar2=bn_shift[:, kc : kc + 1],
-                    op0=ALU.mult,
-                    op1=ALU.add,
-                )
-
         def transpose_z(ch):
             for j in range(PACK):
                 zt[ch, j] = transpose_bank([P, K], F32)
@@ -258,14 +325,17 @@ def tile_modelnew_t_kernel(tc, x, clusters, clusters2, bn_gamma, bn_beta, out):
                         zt[ch, j][:, kc * P : (kc + 1) * P], a_view(ch, kc)[:, j * P : (j + 1) * P], ident_f[:]
                     )
 
+        def row_max(ch, j):
+            if j == 0:
+                neg_max[ch] = stage2.tile([P, PACK], F32, tag="neg_max", name="neg_max")
+            nc.vector.tensor_reduce(
+                out=neg_max[ch][:, j : j + 1], in_=zt[ch, j][:], axis=AXIS_X, op=ALU.max, negate=True
+            )
+
         def exponentials(ch):
             e[ch] = stage2.tile([P, PACK, K], F32, tag="e", name="e", bufs=3)
-            neg_max[ch] = stage2.tile([P, PACK], F32, tag="neg_max", name="neg_max")
             row_sum[ch] = stage2.tile([P, PACK], F32, tag="row_sum", name="row_sum")
             for j in range(PACK):
-                nc.vector.tensor_reduce(
-                    out=neg_max[ch][:, j : j + 1], in_=zt[ch, j][:], axis=AXIS_X, op=ALU.max, negate=True
-                )
                 nc.scalar.activation(
                     out=e[ch][:, j, :],
                     in_=zt[ch, j][:],
@@ -421,12 +491,19 @@ def tile_modelnew_t_kernel(tc, x, clusters, clusters2, bn_gamma, bn_beta, out):
             copy_out(on_vector, out_rows[b, dg][:, tt, :], vt[:])
             nc.sync.dma_start(out=dram_tiles(b)[:, t, :], in_=out_rows[b, dg][:, tt, :])
 
-        normalise(0)
-        normalise(1)
         transpose_z(0)
+        for j in range(PACK):
+            row_max(0, j)
+        quantise_xn(CHUNKS - 1)
+        normalise(1, range(KC))
         for ch in range(CHUNKS + 1):
             if ch < CHUNKS:
+                if ch > 0:
+                    for j in range(PACK):
+                        row_max(ch, j)
                 exponentials(ch)
+            if ch + 2 < CHUNKS:
+                normalise_scalar(ch + 2)
             if ch > 0:
                 round_p(ch - 1)
             if ch < CHUNKS:
@@ -443,12 +520,17 @@ def tile_modelnew_t_kernel(tc, x, clusters, clusters2, bn_gamma, bn_beta, out):
             if ch < CHUNKS:
                 sum_p(ch)
             if ch + 2 < CHUNKS:
-                normalise(ch + 2)
+                normalise_vector(ch + 2)
             if ch > 0:
                 quantise_p(ch - 1)
             if ch == CHUNKS - 1:
                 for kc in range(EARLY):
                     square_sum(0, kc)
+
+        def out_unit(b, unit):
+            dg, half = divmod(unit, 2)
+            transpose_group(b, dg, 2 * half, dg == 1)
+            transpose_group(b, dg, 2 * half + 1, False)
 
         OUT_LAG = 2 * KC - 1
         for step in range(EARLY, B * KC):
@@ -457,29 +539,27 @@ def tile_modelnew_t_kernel(tc, x, clusters, clusters2, bn_gamma, bn_beta, out):
             if b > 0 and kc == 1:
                 add_over_partitions(b - 1)
             if step >= OUT_LAG:
-                out_b, out_kc = divmod(step - OUT_LAG, KC)
-                transpose_group(out_b, 0, out_kc, True)
-                transpose_group(out_b, 1, out_kc, False)
+                out_unit(*divmod(step - OUT_LAG, KC))
             square_sum(b, kc)
             if b > 0 and kc == 0:
                 unit_norms(b - 1)
             if b > 0 and kc == 1:
                 make_factor(b - 1)
-                for scaled in range(KC):
-                    scale_v(b - 1, scaled, nc.gpsimd)
+            ahead = step + 1 - OUT_LAG
+            if ahead >= 0 and ahead % KC < 2:
+                scale_v(ahead // KC, 2 * (ahead % KC), nc.vector)
+                scale_v(ahead // KC, 2 * (ahead % KC) + 1, nc.vector)
         before, last = B - 2, B - 1
-        transpose_group(before, 0, 1, True)
-        transpose_group(before, 1, 1, False)
         unit_norms(last)
-        transpose_group(before, 0, 2, True)
         add_over_partitions(last)
-        transpose_group(before, 1, 2, False)
+        out_unit(before, 1)
         make_factor(last)
-        transpose_group(before, 0, 3, False)
-        transpose_group(before, 1, 3, True)
-        scale_v(last, 0, nc.vector)
-        scale_v(last, 1, nc.vector)
-        scale_v(last, 2, nc.vector)
-        scale_v(last, 3, nc.vector)
+        out_unit(before, 2)
+        out_unit(before, 3)
+        for kc in range(KC - 1):
+            scale_v(last, kc, nc.vector)
+        nc.scalar.activation(
+            out=v[last, KC - 1][:], in_=v[last, KC - 1][:], func=ACT.Copy, scale=factor[last][:, KC - 1 : KC]
+        )
         for t in range(D_TILES):
             transpose_tile(last, t, t % 2 == 0)

@@ -17,12 +17,14 @@ PACK = 4
 K_PASS = P * PACK
 B, N, D, K = 4, 1024, 1024, 512
 ROWS = B * N
+ROOT_ROWS = 64.0
 CHUNK = K_PASS
 CHUNKS = ROWS // CHUNK
 CHUNKS_PER_BATCH = N // CHUNK
 D_PASSES = D // K_PASS
 KC = K // P
 D_TILES = D // P
+STORE_TILES = 2
 EARLY = 2
 NV = (0, 1, 2)
 V_STATS = ((7, 1), (7, 3))
@@ -70,12 +72,12 @@ def tile_modelnew_t_kernel(tc, x, clusters, clusters2, bn_gamma, bn_beta, out):
         xn_codes = [keep.tile([P, D], U32, name="xn_codes%d" % ch, align_bytes=64) for ch in range(CHUNKS)]
         xn_scales = [keep.tile([P, D], U8, name="xn_scales%d" % ch, align_bytes=64) for ch in range(CHUNKS)]
         c2T = keep.tile([P, KC, D], BF16)
-        sum_a = keep.tile([P, KC, CHUNKS], F32)
-        sum_aa = keep.tile([P, KC, CHUNKS], F32)
+        sums = keep.tile([P, 2, KC, CHUNKS], F32)
+        sum_a = sums[:, 0]
+        sum_aa = sums[:, 1]
+        totals = keep.tile([P, 2, KC], F32)
         gamma_beta = keep.tile([P, 2 * KC], F32)
-        mean = keep.tile([P, KC], F32)
-        mean_aa = keep.tile([P, KC], F32)
-        var = keep.tile([P, KC], F32)
+        spread = keep.tile([P, KC], F32)
         rstd = keep.tile([P, KC], F32)
         bn_scale = keep.tile([P, KC], F32)
         bn_shift = keep.tile([P, KC], F32)
@@ -227,12 +229,12 @@ def tile_modelnew_t_kernel(tc, x, clusters, clusters2, bn_gamma, bn_beta, out):
                 )
 
             c_raw = stage1.tile([P, 2 * D_PASSES, 2, K], BF16, bufs=1)
-            load_chunk(0, 2)
             for g in range(D_PASSES):
                 nc.sync.dma_start(
                     out=c_raw[:, 2 * g : 2 * g + 2],
                     in_=clusters[g * K_PASS : (g + 1) * K_PASS].rearrange("(u q e) k -> q u e k", u=2, e=2),
                 )
+            load_chunk(0, 2)
             for ch in range(1, X_BUFS):
                 load_chunk(ch)
             gb_rows = stage1.tile([P, P], BF16, bufs=1)
@@ -261,8 +263,8 @@ def tile_modelnew_t_kernel(tc, x, clusters, clusters2, bn_gamma, bn_beta, out):
             group_clusters(0)
             group_clusters(1)
             quantise_clusters(0)
-            quantise_xd(0)
             quantise_clusters(1)
+            quantise_xd(0)
 
             for ch in range(CHUNKS):
                 if ch + 1 < CHUNKS:
@@ -289,19 +291,23 @@ def tile_modelnew_t_kernel(tc, x, clusters, clusters2, bn_gamma, bn_beta, out):
                     )
                 nc.scalar.copy(out=c2T[:, kc, :], in_=c2_ps[:])
 
-            nc.vector.tensor_reduce(out=mean[:], in_=sum_a[:], axis=AXIS_X, op=ALU.add)
-            nc.vector.tensor_reduce(out=mean_aa[:], in_=sum_aa[:], axis=AXIS_X, op=ALU.add)
-            nc.vector.tensor_scalar(out=mean[:], in0=mean[:], scalar1=1.0 / ROWS, scalar2=None, op0=ALU.mult)
-            nc.vector.tensor_tensor(out=var[:], in0=mean[:], in1=mean[:], op=ALU.mult)
+            nc.vector.tensor_reduce(out=totals[:], in_=sums[:], axis=AXIS_X, op=ALU.add)
             nc.vector.scalar_tensor_tensor(
-                out=var[:], in0=mean_aa[:], scalar=1.0 / ROWS, in1=var[:], op0=ALU.mult, op1=ALU.subtract
+                out=spread[:], in0=totals[:, 0], scalar=-1.0 / ROWS, in1=totals[:, 0], op0=ALU.mult, op1=ALU.mult
             )
-            nc.vector.tensor_scalar(out=var[:], in0=var[:], scalar1=0.0, scalar2=BN_EPS, op0=ALU.max, op1=ALU.add)
-            nc.gpsimd.tensor_tensor(out=rstd[:], in0=var[:], in1=neg_half[:], op=ALU.pow)
+            nc.vector.tensor_tensor(out=spread[:], in0=spread[:], in1=totals[:, 1], op=ALU.add)
+            nc.vector.tensor_scalar(
+                out=spread[:], in0=spread[:], scalar1=0.0, scalar2=ROWS * BN_EPS, op0=ALU.max, op1=ALU.add
+            )
+            nc.gpsimd.tensor_tensor(out=rstd[:], in0=spread[:], in1=neg_half[:], op=ALU.pow)
             regroup_xn(CHUNKS - 1, range(0, 2))
-            nc.vector.tensor_tensor(out=bn_scale[:], in0=gamma_beta[:, 0:KC], in1=rstd[:], op=ALU.mult)
-            nc.vector.tensor_tensor(out=bn_shift[:], in0=mean[:], in1=bn_scale[:], op=ALU.mult)
-            nc.vector.tensor_tensor(out=bn_shift[:], in0=gamma_beta[:, KC : 2 * KC], in1=bn_shift[:], op=ALU.subtract)
+            nc.vector.scalar_tensor_tensor(
+                out=bn_scale[:], in0=rstd[:], scalar=ROOT_ROWS, in1=gamma_beta[:, 0:KC], op0=ALU.mult, op1=ALU.mult
+            )
+            nc.vector.scalar_tensor_tensor(
+                out=bn_shift[:], in0=totals[:, 0], scalar=-1.0 / ROWS, in1=bn_scale[:], op0=ALU.mult, op1=ALU.mult
+            )
+            nc.vector.tensor_tensor(out=bn_shift[:], in0=gamma_beta[:, KC : 2 * KC], in1=bn_shift[:], op=ALU.add)
 
             normalise(0, (1, 3))
             regroup_xn(CHUNKS - 1, range(2, 4))
@@ -436,9 +442,20 @@ def tile_modelnew_t_kernel(tc, x, clusters, clusters2, bn_gamma, bn_beta, out):
             nc.vector.tensor_scalar(
                 out=floored[b][:], in0=sum_vv[b][:], scalar1=NORM_EPS * NORM_EPS, scalar2=None, op0=ALU.max
             )
+            if b == B - 1:
+                nc.gpsimd.tensor_tensor(out=own_norm[:], in0=floored[b][:], in1=neg_half[:], op=ALU.pow)
             nc.vector.reciprocal(out=unit[:], in_=floored[b][:])
             nc.vector.tensor_tensor(out=unit[:], in0=unit[:], in1=sum_vv[b][:], op=ALU.mult)
             nc.vector.tensor_reduce(out=unit_sum[b][:], in_=unit[:], axis=AXIS_X, op=ALU.add)
+
+        own_norm = keep.tile([P, KC], F32)
+        row_norm = keep.tile([P, 1], F32)
+
+        def invert_row_norm(b):
+            nc.vector.tensor_scalar(
+                out=row_norm[:], in0=total_ps[b][:], scalar1=NORM_EPS * NORM_EPS, scalar2=None, op0=ALU.max
+            )
+            nc.gpsimd.tensor_tensor(out=row_norm[:], in0=row_norm[:], in1=neg_half[:, 0:1], op=ALU.pow)
 
         def add_over_partitions(b):
             total_ps[b] = psum.tile([P, 1], F32, tag="small", name="total")
@@ -481,6 +498,15 @@ def tile_modelnew_t_kernel(tc, x, clusters, clusters2, bn_gamma, bn_beta, out):
                 tiles = slice(dg * HALF_TILES, (dg + 1) * HALF_TILES)
                 nc.sync.dma_start(out=dram_tiles(b)[:, tiles, :], in_=out_rows[b, dg][:])
 
+        def scale_own(kc, on_vector):
+            v_last = v[B - 1, kc][:]
+            if on_vector:
+                nc.vector.tensor_scalar(
+                    out=v_last, in0=v_last, scalar1=own_norm[:, kc : kc + 1], scalar2=None, op0=ALU.mult
+                )
+            else:
+                nc.scalar.activation(out=v_last, in_=v_last, func=ACT.Copy, scale=own_norm[:, kc : kc + 1])
+
         def transpose_tile(b, t, on_vector):
             dg, tt = divmod(t, HALF_TILES)
             if tt == 0:
@@ -488,8 +514,17 @@ def tile_modelnew_t_kernel(tc, x, clusters, clusters2, bn_gamma, bn_beta, out):
             vt = transpose_bank([P, K], F32)
             for kc in range(KC):
                 nc.tensor.transpose(vt[:, kc * P : (kc + 1) * P], v[b, kc][:, t * P : (t + 1) * P], ident_f[:])
-            copy_out(on_vector, out_rows[b, dg][:, tt, :], vt[:])
-            nc.sync.dma_start(out=dram_tiles(b)[:, t, :], in_=out_rows[b, dg][:, tt, :])
+            if on_vector:
+                nc.vector.tensor_scalar(
+                    out=out_rows[b, dg][:, tt, :], in0=vt[:], scalar1=row_norm[:, 0:1], scalar2=None, op0=ALU.mult
+                )
+            else:
+                nc.scalar.activation(out=out_rows[b, dg][:, tt, :], in_=vt[:], func=ACT.Copy, scale=row_norm[:, 0:1])
+            if tt % STORE_TILES == STORE_TILES - 1:
+                ts = slice(t - STORE_TILES + 1, t + 1)
+                nc.sync.dma_start(
+                    out=dram_tiles(b)[:, ts, :], in_=out_rows[b, dg][:, tt - STORE_TILES + 1 : tt + 1, :]
+                )
 
         transpose_z(0)
         for j in range(PACK):
@@ -551,15 +586,14 @@ def tile_modelnew_t_kernel(tc, x, clusters, clusters2, bn_gamma, bn_beta, out):
                 scale_v(ahead // KC, 2 * (ahead % KC) + 1, nc.vector)
         before, last = B - 2, B - 1
         unit_norms(last)
-        add_over_partitions(last)
         out_unit(before, 1)
-        make_factor(last)
+        add_over_partitions(last)
+        scale_own(0, True)
+        scale_own(2, False)
+        invert_row_norm(last)
+        scale_own(1, True)
+        scale_own(3, False)
         out_unit(before, 2)
         out_unit(before, 3)
-        for kc in range(KC - 1):
-            scale_v(last, kc, nc.vector)
-        nc.scalar.activation(
-            out=v[last, KC - 1][:], in_=v[last, KC - 1][:], func=ACT.Copy, scale=factor[last][:, KC - 1 : KC]
-        )
         for t in range(D_TILES):
             transpose_tile(last, t, t % 2 == 0)

@@ -248,8 +248,8 @@ def tile_modelnew_t_kernel(tc, x, clusters, clusters2, bn_gamma, bn_beta, out):
 
             def group_clusters(g):
                 nc.vector.tensor_copy(
-                    out=c_grouped[:, g].rearrange("q k (u e) -> q k u e", e=2),
-                    in_=c_raw[:, 2 * g : 2 * g + 2].rearrange("q u e k -> q k u e"),
+                    out=c_grouped[:, g].rearrange("q (s i) t -> q s t i", i=4),
+                    in_=c_raw[:, 2 * g : 2 * g + 2].rearrange("q u e (s i) -> q s (u e) i", i=4),
                 )
 
             def quantise_clusters(g):
@@ -383,7 +383,10 @@ def tile_modelnew_t_kernel(tc, x, clusters, clusters2, bn_gamma, bn_beta, out):
 
         def round_p(ch):
             p_grouped[ch] = stage2.tile([P, K, PACK], BF16, tag="p_grouped", name="p_grouped", align_bytes=64)
-            nc.vector.tensor_copy(out=p_grouped[ch][:], in_=e[ch][:].rearrange("q j k -> q k j"))
+            nc.vector.tensor_copy(
+                out=p_grouped[ch][:].rearrange("q (s i) j -> q s j i", i=4),
+                in_=e[ch][:].rearrange("q j (s i) -> q s j i", i=4),
+            )
 
         def quantise_p(ch):
             p_codes[ch] = stage2.tile([P, K], U32, tag="p_codes", name="p_codes", bufs=CHUNKS, align_bytes=64)

@@ -27,7 +27,6 @@ D_TILES = D // P
 STORE_TILES = 2
 EARLY = 2
 NV = (0, 1, 2)
-V_STATS = ((7, 1), (7, 3))
 V_XCP = [(ch, j) for ch in range(1, 8) for j in ((1, 3) if ch < 6 else (0, 1, 3))]
 BANK = 512
 BN_EPS = 1e-5
@@ -79,6 +78,7 @@ def tile_modelnew_t_kernel(tc, x, clusters, clusters2, bn_gamma, bn_beta, out):
         gamma_beta = keep.tile([P, 2 * KC], F32)
         spread = keep.tile([P, KC], F32)
         rstd = keep.tile([P, KC], F32)
+        gamma_mean = keep.tile([P, KC], F32)
         bn_scale = keep.tile([P, KC], F32)
         bn_shift = keep.tile([P, KC], F32)
         neg_a_sum = keep.tile([P, B, KC], F32)
@@ -190,16 +190,10 @@ def tile_modelnew_t_kernel(tc, x, clusters, clusters2, bn_gamma, bn_beta, out):
                             stop=(g == D_PASSES - 1),
                         )
                     squares = scrap.tile([P, D], BF16, tag="squares")
-                    if (ch, kc) in V_STATS:
-                        nc.vector.tensor_scalar(
-                            out=a_view(ch, kc),
-                            in0=acc[:],
-                            scalar1=1.0,
-                            scalar2=None,
-                            op0=ALU.mult,
-                            op1=ALU.add,
-                            accum_out=sum_a[:, kc, ch : ch + 1],
-                        )
+                    nc.scalar.activation(
+                        out=a_view(ch, kc), in_=acc[:], func=ACT.Identity, accum_out=sum_a[:, kc, ch : ch + 1]
+                    )
+                    if ch == CHUNKS - 1:
                         nc.vector.scalar_tensor_tensor(
                             out=squares[:, 0:CHUNK],
                             in0=acc[:],
@@ -210,9 +204,6 @@ def tile_modelnew_t_kernel(tc, x, clusters, clusters2, bn_gamma, bn_beta, out):
                             accum_out=sum_aa[:, kc, ch : ch + 1],
                         )
                     else:
-                        nc.scalar.activation(
-                            out=a_view(ch, kc), in_=acc[:], func=ACT.Identity, accum_out=sum_a[:, kc, ch : ch + 1]
-                        )
                         nc.scalar.activation(
                             out=squares[:, 0:CHUNK], in_=acc[:], func=ACT.Square, accum_out=sum_aa[:, kc, ch : ch + 1]
                         )
@@ -300,12 +291,18 @@ def tile_modelnew_t_kernel(tc, x, clusters, clusters2, bn_gamma, bn_beta, out):
                 out=spread[:], in0=spread[:], scalar1=0.0, scalar2=ROWS * BN_EPS, op0=ALU.max, op1=ALU.add
             )
             nc.gpsimd.tensor_tensor(out=rstd[:], in0=spread[:], in1=neg_half[:], op=ALU.pow)
+            nc.vector.scalar_tensor_tensor(
+                out=gamma_mean[:],
+                in0=totals[:, 0],
+                scalar=-ROOT_ROWS / ROWS,
+                in1=gamma_beta[:, 0:KC],
+                op0=ALU.mult,
+                op1=ALU.mult,
+            )
             regroup_xn(CHUNKS - 1, range(0, 2))
+            nc.vector.tensor_tensor(out=bn_shift[:], in0=gamma_mean[:], in1=rstd[:], op=ALU.mult)
             nc.vector.scalar_tensor_tensor(
                 out=bn_scale[:], in0=rstd[:], scalar=ROOT_ROWS, in1=gamma_beta[:, 0:KC], op0=ALU.mult, op1=ALU.mult
-            )
-            nc.vector.scalar_tensor_tensor(
-                out=bn_shift[:], in0=totals[:, 0], scalar=-1.0 / ROWS, in1=bn_scale[:], op0=ALU.mult, op1=ALU.mult
             )
             nc.vector.tensor_tensor(out=bn_shift[:], in0=gamma_beta[:, KC : 2 * KC], in1=bn_shift[:], op=ALU.add)
 
@@ -400,7 +397,7 @@ def tile_modelnew_t_kernel(tc, x, clusters, clusters2, bn_gamma, bn_beta, out):
         v = {}
         sum_vv = {}
         floored = {}
-        unit_sum = {}
+        unit = {}
         total_ps = {}
         factor = {}
         out_rows = {}
@@ -439,17 +436,21 @@ def tile_modelnew_t_kernel(tc, x, clusters, clusters2, bn_gamma, bn_beta, out):
             nc.scalar.activation(out=squares[:], in_=v[b, kc][:], func=ACT.Square, accum_out=sum_vv[b][:, kc : kc + 1])
 
         def unit_norms(b):
+            unit[b] = stage2.tile([P, KC], F32, tag="unit", name="unit")
             floored[b] = stage2.tile([P, KC], F32, tag="floored", name="floored")
-            unit = stage2.tile([P, KC], F32, tag="unit")
-            unit_sum[b] = stage2.tile([P, 1], F32, tag="unit_sum", name="unit_sum")
+            nc.vector.tensor_scalar(
+                out=unit[b][:],
+                in0=sum_vv[b][:],
+                scalar1=1.0 / (NORM_EPS * NORM_EPS),
+                scalar2=1.0,
+                op0=ALU.mult,
+                op1=ALU.min,
+            )
             nc.vector.tensor_scalar(
                 out=floored[b][:], in0=sum_vv[b][:], scalar1=NORM_EPS * NORM_EPS, scalar2=None, op0=ALU.max
             )
             if b == B - 1:
                 nc.gpsimd.tensor_tensor(out=own_norm[:], in0=floored[b][:], in1=neg_half[:], op=ALU.pow)
-            nc.vector.reciprocal(out=unit[:], in_=floored[b][:])
-            nc.vector.tensor_tensor(out=unit[:], in0=unit[:], in1=sum_vv[b][:], op=ALU.mult)
-            nc.vector.tensor_reduce(out=unit_sum[b][:], in_=unit[:], axis=AXIS_X, op=ALU.add)
 
         own_norm = keep.tile([P, KC], F32)
         row_norm = keep.tile([P, 1], F32)
@@ -462,7 +463,14 @@ def tile_modelnew_t_kernel(tc, x, clusters, clusters2, bn_gamma, bn_beta, out):
 
         def add_over_partitions(b):
             total_ps[b] = psum.tile([P, 1], F32, tag="small", name="total")
-            nc.tensor.matmul(out=total_ps[b][:], lhsT=ones_f[:], rhs=unit_sum[b][:], start=True, stop=True)
+            for kc in range(KC):
+                nc.tensor.matmul(
+                    out=total_ps[b][:],
+                    lhsT=ones_f[:],
+                    rhs=unit[b][:, kc : kc + 1],
+                    start=(kc == 0),
+                    stop=(kc == KC - 1),
+                )
 
         def make_factor(b):
             factor[b] = stage2.tile([P, KC], F32, tag="factor", name="factor")
@@ -530,10 +538,13 @@ def tile_modelnew_t_kernel(tc, x, clusters, clusters2, bn_gamma, bn_beta, out):
                 )
 
         transpose_z(0)
+        for kc in (0, 1):
+            normalise_group(1, kc, False)
         for j in range(PACK):
             row_max(0, j)
+        for kc in (2, 3):
+            normalise_group(1, kc, True)
         quantise_xn(CHUNKS - 1)
-        normalise(1, range(KC))
         for ch in range(CHUNKS + 1):
             if ch < CHUNKS:
                 if ch > 0:
@@ -589,14 +600,17 @@ def tile_modelnew_t_kernel(tc, x, clusters, clusters2, bn_gamma, bn_beta, out):
                 scale_v(ahead // KC, 2 * (ahead % KC) + 1, nc.vector)
         before, last = B - 2, B - 1
         unit_norms(last)
-        out_unit(before, 1)
+        for kc in (2, 3):
+            transpose_group(before, 0, kc, False)
         add_over_partitions(last)
+        transpose_group(before, 1, 0, True)
+        invert_row_norm(last)
+        transpose_group(before, 1, 1, True)
+        transpose_group(before, 1, 2, False)
+        transpose_group(before, 1, 3, False)
         scale_own(0, True)
         scale_own(2, False)
-        invert_row_norm(last)
         scale_own(1, True)
-        scale_own(3, False)
-        out_unit(before, 2)
-        out_unit(before, 3)
+        scale_own(3, True)
         for t in range(D_TILES):
             transpose_tile(last, t, t % 2 == 0)

@@ -398,6 +398,7 @@ def tile_modelnew_t_kernel(tc, x, clusters, clusters2, bn_gamma, bn_beta, out):
         sum_vv = {}
         floored = {}
         unit = {}
+        unit_sum = {}
         total_ps = {}
         factor = {}
         out_rows = {}
@@ -449,6 +450,8 @@ def tile_modelnew_t_kernel(tc, x, clusters, clusters2, bn_gamma, bn_beta, out):
             nc.vector.tensor_scalar(
                 out=floored[b][:], in0=sum_vv[b][:], scalar1=NORM_EPS * NORM_EPS, scalar2=None, op0=ALU.max
             )
+            unit_sum[b] = stage2.tile([P, 1], F32, tag="unit_sum", name="unit_sum")
+            nc.vector.tensor_reduce(out=unit_sum[b][:], in_=unit[b][:], axis=AXIS_X, op=ALU.add)
             if b == B - 1:
                 nc.gpsimd.tensor_tensor(out=own_norm[:], in0=floored[b][:], in1=neg_half[:], op=ALU.pow)
 
@@ -463,14 +466,7 @@ def tile_modelnew_t_kernel(tc, x, clusters, clusters2, bn_gamma, bn_beta, out):
 
         def add_over_partitions(b):
             total_ps[b] = psum.tile([P, 1], F32, tag="small", name="total")
-            for kc in range(KC):
-                nc.tensor.matmul(
-                    out=total_ps[b][:],
-                    lhsT=ones_f[:],
-                    rhs=unit[b][:, kc : kc + 1],
-                    start=(kc == 0),
-                    stop=(kc == KC - 1),
-                )
+            nc.tensor.matmul(out=total_ps[b][:], lhsT=ones_f[:], rhs=unit_sum[b][:], start=True, stop=True)
 
         def make_factor(b):
             factor[b] = stage2.tile([P, KC], F32, tag="factor", name="factor")

@@ -194,6 +194,8 @@ def tile_modelnew_t_kernel(tc, x, clusters, clusters2, bn_gamma, bn_beta, out):
                         out=a_view(ch, kc), in_=acc[:], func=ACT.Identity, accum_out=sum_a[:, kc, ch : ch + 1]
                     )
                     if ch == CHUNKS - 1:
+                        if kc == KC - 1:
+                            add_up(0)
                         nc.vector.scalar_tensor_tensor(
                             out=squares[:, 0:CHUNK],
                             in0=acc[:],
@@ -208,15 +210,19 @@ def tile_modelnew_t_kernel(tc, x, clusters, clusters2, bn_gamma, bn_beta, out):
                             out=squares[:, 0:CHUNK], in_=acc[:], func=ACT.Square, accum_out=sum_aa[:, kc, ch : ch + 1]
                         )
 
-            def regroup_xn(ch, parts):
+            def add_up(which):
+                nc.vector.tensor_reduce(out=totals[:, which], in_=sums[:, which], axis=AXIS_X, op=ALU.add)
+
+            def regroup_xn(ch, parts, on_vector=True):
                 if parts.start == 0:
                     xn_grouped[ch] = scrap.tile(
                         [P, D * PACK], BF16, tag="xn_grouped", name="xn_grouped", align_bytes=64
                     )
                 s = slice(parts.start * D // 16, parts.stop * D // 16)
-                nc.vector.tensor_copy(
-                    out=xn_grouped[ch][:].rearrange("q (s i j) -> q s j i", i=4, j=PACK)[:, s],
-                    in_=x_tiles[ch][:].rearrange("q (j s i) -> q s j i", j=PACK, i=4)[:, s],
+                copy_out(
+                    on_vector,
+                    xn_grouped[ch][:].rearrange("q (s i j) -> q s j i", i=4, j=PACK)[:, s],
+                    x_tiles[ch][:].rearrange("q (j s i) -> q s j i", j=PACK, i=4)[:, s],
                 )
 
             c_raw = stage1.tile([P, 2 * D_PASSES, 2, K], BF16, bufs=1)
@@ -251,6 +257,7 @@ def tile_modelnew_t_kernel(tc, x, clusters, clusters2, bn_gamma, bn_beta, out):
                 )
 
             transpose_chunk(0)
+            regroup_xn(0, range(0, 1), on_vector=False)
             group_clusters(0)
             group_clusters(1)
             quantise_clusters(0)
@@ -260,17 +267,17 @@ def tile_modelnew_t_kernel(tc, x, clusters, clusters2, bn_gamma, bn_beta, out):
             for ch in range(CHUNKS):
                 if ch + 1 < CHUNKS:
                     transpose_chunk(ch + 1)
+                if ch == CHUNKS - 1:
+                    gb_ps = transpose_bank([P, P], BF16)
+                    nc.tensor.transpose(gb_ps[:], gb_rows[:], ident_b[:])
+                    nc.vector.tensor_copy(out=gamma_beta[:], in_=gb_ps[:, 0 : 2 * KC])
                 first_matmul(ch)
                 if ch + 1 < CHUNKS:
-                    regroup_xn(ch, range(0, 4))
+                    regroup_xn(ch, range(1 if ch == 0 else 0, 4))
                     quantise_xd(ch + 1)
                     quantise_xn(ch)
                 if ch + X_BUFS < CHUNKS:
                     load_chunk(ch + X_BUFS)
-
-            gb_ps = transpose_bank([P, P], BF16)
-            nc.tensor.transpose(gb_ps[:], gb_rows[:], ident_b[:])
-            nc.vector.tensor_copy(out=gamma_beta[:], in_=gb_ps[:, 0 : 2 * KC])
 
             c2_raw = stage1.tile([P, D_TILES, K], BF16, bufs=1)
             nc.sync.dma_start(out=c2_raw[:], in_=clusters2[0].rearrange("(t q) k -> q t k", q=P))
@@ -282,15 +289,10 @@ def tile_modelnew_t_kernel(tc, x, clusters, clusters2, bn_gamma, bn_beta, out):
                     )
                 nc.scalar.copy(out=c2T[:, kc, :], in_=c2_ps[:])
 
-            nc.vector.tensor_reduce(out=totals[:], in_=sums[:], axis=AXIS_X, op=ALU.add)
             nc.vector.scalar_tensor_tensor(
                 out=spread[:], in0=totals[:, 0], scalar=-1.0 / ROWS, in1=totals[:, 0], op0=ALU.mult, op1=ALU.mult
             )
-            nc.vector.tensor_tensor(out=spread[:], in0=spread[:], in1=totals[:, 1], op=ALU.add)
-            nc.vector.tensor_scalar(
-                out=spread[:], in0=spread[:], scalar1=0.0, scalar2=ROWS * BN_EPS, op0=ALU.max, op1=ALU.add
-            )
-            nc.gpsimd.tensor_tensor(out=rstd[:], in0=spread[:], in1=neg_half[:], op=ALU.pow)
+            add_up(1)
             nc.vector.scalar_tensor_tensor(
                 out=gamma_mean[:],
                 in0=totals[:, 0],
@@ -299,7 +301,13 @@ def tile_modelnew_t_kernel(tc, x, clusters, clusters2, bn_gamma, bn_beta, out):
                 op0=ALU.mult,
                 op1=ALU.mult,
             )
+            nc.vector.tensor_tensor(out=spread[:], in0=spread[:], in1=totals[:, 1], op=ALU.add)
+            nc.vector.tensor_scalar(
+                out=spread[:], in0=spread[:], scalar1=0.0, scalar2=ROWS * BN_EPS, op0=ALU.max, op1=ALU.add
+            )
+            nc.gpsimd.tensor_tensor(out=rstd[:], in0=spread[:], in1=neg_half[:], op=ALU.pow)
             regroup_xn(CHUNKS - 1, range(0, 2))
+            regroup_xn(CHUNKS - 1, range(2, 3), on_vector=False)
             nc.vector.tensor_tensor(out=bn_shift[:], in0=gamma_mean[:], in1=rstd[:], op=ALU.mult)
             nc.vector.scalar_tensor_tensor(
                 out=bn_scale[:], in0=rstd[:], scalar=ROOT_ROWS, in1=gamma_beta[:, 0:KC], op0=ALU.mult, op1=ALU.mult
@@ -307,7 +315,7 @@ def tile_modelnew_t_kernel(tc, x, clusters, clusters2, bn_gamma, bn_beta, out):
             nc.vector.tensor_tensor(out=bn_shift[:], in0=gamma_beta[:, KC : 2 * KC], in1=bn_shift[:], op=ALU.add)
 
             normalise(0, (1, 3))
-            regroup_xn(CHUNKS - 1, range(2, 4))
+            regroup_xn(CHUNKS - 1, range(3, 4))
 
         stage2 = ctx.enter_context(tc.tile_pool(name="stage2", bufs=2, reuse_waits="tile"))
         zt = {}
@@ -534,11 +542,11 @@ def tile_modelnew_t_kernel(tc, x, clusters, clusters2, bn_gamma, bn_beta, out):
                 )
 
         transpose_z(0)
-        for kc in (0, 1):
+        for kc in (0, 1, 2):
             normalise_group(1, kc, False)
         for j in range(PACK):
             row_max(0, j)
-        for kc in (2, 3):
+        for kc in (3,):
             normalise_group(1, kc, True)
         quantise_xn(CHUNKS - 1)
         for ch in range(CHUNKS + 1):
@@ -574,7 +582,7 @@ def tile_modelnew_t_kernel(tc, x, clusters, clusters2, bn_gamma, bn_beta, out):
 
         def out_unit(b, unit):
             dg, half = divmod(unit, 2)
-            transpose_group(b, dg, 2 * half, dg == 1)
+            transpose_group(b, dg, 2 * half, unit == 2)
             transpose_group(b, dg, 2 * half + 1, False)
 
         OUT_LAG = 2 * KC - 1

@@ -68,8 +68,8 @@ def tile_modelnew_t_kernel(tc, x, clusters, clusters2, bn_gamma, bn_beta, out):
         nc.vector.memset(warm[:], 0.0)
         nc.scalar.activation(out=warm[:], in_=warm[:], func=ACT.Exp)
 
-        xn_codes = [keep.tile([P, D], U32, name="xn_codes%d" % ch, align_bytes=64) for ch in range(CHUNKS)]
-        xn_scales = [keep.tile([P, D], U8, name="xn_scales%d" % ch, align_bytes=64) for ch in range(CHUNKS)]
+        xn_codes = [keep.tile([P, D], U32, name="xn_codes%d" % ch, align_bytes=256) for ch in range(CHUNKS)]
+        xn_scales = [keep.tile([P, D], U8, name="xn_scales%d" % ch, align_bytes=256) for ch in range(CHUNKS)]
         c2T = keep.tile([P, KC, D], BF16)
         sums = keep.tile([P, 2, KC, CHUNKS], F32)
         sum_a = sums[:, 0]
@@ -147,7 +147,7 @@ def tile_modelnew_t_kernel(tc, x, clusters, clusters2, bn_gamma, bn_beta, out):
             def transpose_chunk(ch):
                 x_words = x_tiles[ch][:].bitcast(F32)
                 xd_grouped[ch] = stage1.tile(
-                    [P, D_PASSES * CHUNK * PACK], BF16, tag="xd_grouped", name="xd_grouped", align_bytes=64
+                    [P, D_PASSES * CHUNK * PACK], BF16, tag="xd_grouped", name="xd_grouped", align_bytes=256
                 )
                 xd_words = xd_grouped[ch][:].bitcast(F32).rearrange("q (g n u) -> q g n u", g=D_PASSES, u=2)
                 for j in range(PACK):
@@ -163,10 +163,10 @@ def tile_modelnew_t_kernel(tc, x, clusters, clusters2, bn_gamma, bn_beta, out):
 
             def quantise_xd(ch):
                 xd_codes[ch] = stage1.tile(
-                    [P, D_PASSES * CHUNK], U32, tag="xd_codes", name="xd_codes", align_bytes=64
+                    [P, D_PASSES * CHUNK], U32, tag="xd_codes", name="xd_codes", align_bytes=256
                 )
                 xd_scales[ch] = stage1.tile(
-                    [P, D_PASSES * CHUNK], U8, tag="xd_scales", name="xd_scales", align_bytes=64
+                    [P, D_PASSES * CHUNK], U8, tag="xd_scales", name="xd_scales", align_bytes=256
                 )
                 nc.vector.quantize_mx(
                     out=xd_codes[ch][:].bitcast(FP8X4), scales=xd_scales[ch][:], in_=xd_grouped[ch][:]
@@ -216,7 +216,7 @@ def tile_modelnew_t_kernel(tc, x, clusters, clusters2, bn_gamma, bn_beta, out):
             def regroup_xn(ch, parts, on_vector=True):
                 if parts.start == 0:
                     xn_grouped[ch] = scrap.tile(
-                        [P, D * PACK], BF16, tag="xn_grouped", name="xn_grouped", align_bytes=64
+                        [P, D * PACK], BF16, tag="xn_grouped", name="xn_grouped", align_bytes=256
                     )
                 s = slice(parts.start * D // 16, parts.stop * D // 16)
                 copy_out(
@@ -239,9 +239,9 @@ def tile_modelnew_t_kernel(tc, x, clusters, clusters2, bn_gamma, bn_beta, out):
             nc.sync.dma_start(out=gb_rows[0:KC, :], in_=bn_gamma.rearrange("(r k) -> r k", k=P))
             nc.sync.dma_start(out=gb_rows[KC : 2 * KC, :], in_=bn_beta.rearrange("(r k) -> r k", k=P))
 
-            c_grouped = stage1.tile([P, D_PASSES, K, PACK], BF16, bufs=1, align_bytes=64)
-            c_codes = stage1.tile([P, D_PASSES * K], U32, bufs=1, align_bytes=64)
-            c_scales = stage1.tile([P, D_PASSES * K], U8, bufs=1, align_bytes=64)
+            c_grouped = stage1.tile([P, D_PASSES, K, PACK], BF16, bufs=1, align_bytes=256)
+            c_codes = stage1.tile([P, D_PASSES * K], U32, bufs=1, align_bytes=256)
+            c_scales = stage1.tile([P, D_PASSES * K], U8, bufs=1, align_bytes=256)
 
             def group_clusters(g):
                 nc.vector.tensor_copy(
@@ -378,6 +378,17 @@ def tile_modelnew_t_kernel(tc, x, clusters, clusters2, bn_gamma, bn_beta, out):
                     )
 
         def negate_a_sum(b):
+            if b == B - 1:
+                for kc in range(KC):
+                    addends = scrap.tile([P, D], BF16, tag="squares", name="addends")
+                    nc.scalar.activation(
+                        out=addends[:, 0:P],
+                        in_=a_sum_ps[b][:, kc * P : (kc + 1) * P],
+                        func=ACT.Copy,
+                        scale=-1.0,
+                        accum_out=neg_a_sum[:, b, kc : kc + 1],
+                    )
+                return
             nc.vector.tensor_reduce(
                 out=neg_a_sum[:, b, :],
                 in_=a_sum_ps[b][:].rearrange("k (kc n) -> k kc n", kc=KC),
@@ -387,15 +398,15 @@ def tile_modelnew_t_kernel(tc, x, clusters, clusters2, bn_gamma, bn_beta, out):
             )
 
         def round_p(ch):
-            p_grouped[ch] = stage2.tile([P, K, PACK], BF16, tag="p_grouped", name="p_grouped", align_bytes=64)
+            p_grouped[ch] = stage2.tile([P, K, PACK], BF16, tag="p_grouped", name="p_grouped", align_bytes=256)
             nc.vector.tensor_copy(
                 out=p_grouped[ch][:].rearrange("q (s i) j -> q s j i", i=4),
                 in_=e[ch][:].rearrange("q j (s i) -> q s j i", i=4),
             )
 
         def quantise_p(ch):
-            p_codes[ch] = stage2.tile([P, K], U32, tag="p_codes", name="p_codes", bufs=CHUNKS, align_bytes=64)
-            p_scales[ch] = stage2.tile([P, K], U8, tag="p_scales", name="p_scales", bufs=CHUNKS, align_bytes=64)
+            p_codes[ch] = stage2.tile([P, K], U32, tag="p_codes", name="p_codes", bufs=CHUNKS, align_bytes=256)
+            p_scales[ch] = stage2.tile([P, K], U8, tag="p_scales", name="p_scales", bufs=CHUNKS, align_bytes=256)
             nc.vector.quantize_mx(
                 out=p_codes[ch][:].bitcast(FP8X4),
                 scales=p_scales[ch][:],
@@ -488,14 +499,9 @@ def tile_modelnew_t_kernel(tc, x, clusters, clusters2, bn_gamma, bn_beta, out):
             )
             nc.gpsimd.tensor_tensor(out=factor[b][:], in0=factor[b][:], in1=neg_half[:], op=ALU.pow)
 
-        def scale_v(b, kc, engine):
-            engine.tensor_scalar(
-                out=v[b, kc][:],
-                in0=v[b, kc][:],
-                scalar1=factor[b][:, kc : kc + 1],
-                scalar2=0.0,
-                op0=ALU.mult,
-                op1=ALU.add,
+        def scale_v(b, kc):
+            nc.vector.tensor_scalar(
+                out=v[b, kc][:], in0=v[b, kc][:], scalar1=factor[b][:, kc : kc + 1], scalar2=None, op0=ALU.mult
             )
 
         def dram_tiles(b):
@@ -600,8 +606,8 @@ def tile_modelnew_t_kernel(tc, x, clusters, clusters2, bn_gamma, bn_beta, out):
                 make_factor(b - 1)
             ahead = step + 1 - OUT_LAG
             if ahead >= 0 and ahead % KC < 2:
-                scale_v(ahead // KC, 2 * (ahead % KC), nc.vector)
-                scale_v(ahead // KC, 2 * (ahead % KC) + 1, nc.vector)
+                scale_v(ahead // KC, 2 * (ahead % KC))
+                scale_v(ahead // KC, 2 * (ahead % KC) + 1)
         before, last = B - 2, B - 1
         unit_norms(last)
         for kc in (2, 3):

from contextlib import ExitStack

import concourse.mybir as mybir
from concourse.masks import make_identity

F32 = mybir.dt.float32
BF16 = mybir.dt.bfloat16
U32 = mybir.dt.uint32
U8 = mybir.dt.uint8
FP8X4 = mybir.dt.float8_e4m3fn_x4
ALU = mybir.AluOpType
ACT = mybir.ActivationFunctionType
AXIS_X = mybir.AxisListType.X

P = 128
PACK = 4
K_PASS = P * PACK
B, N, D, K = 4, 1024, 1024, 512
ROWS = B * N
ROOT_ROWS = 64.0
CHUNK = K_PASS
CHUNKS = ROWS // CHUNK
CHUNKS_PER_BATCH = N // CHUNK
D_PASSES = D // K_PASS
KC = K // P
D_TILES = D // P
STORE_TILES = 2
EARLY = 2
NV = (0, 1, 2)
V_XCP = [(ch, j) for ch in range(1, 8) for j in ((1, 3) if ch < 6 else (0, 1, 3))]
BANK = 512
BN_EPS = 1e-5
NORM_EPS = 1e-12

FLOPS = 2 * ROWS * D * K * 2


def tile_modelnew_t_kernel(tc, x, clusters, clusters2, bn_gamma, bn_beta, out):
    nc = tc.nc
    with ExitStack() as ctx:
        ctx.enter_context(tc.manual_schedule())
        keep = ctx.enter_context(tc.tile_pool(name="keep", bufs=1))
        wide = ctx.enter_context(tc.tile_pool(name="wide", bufs=2 * CHUNKS))
        scrap = ctx.enter_context(tc.tile_pool(name="scrap", bufs=2))
        psum = ctx.enter_context(tc.psum_pool(name="psum", bufs=1))

        def transpose_bank(shape, dtype):
            return psum.tile(shape, dtype, tag="transposed", name="transposed", bufs=4)

        def sum_bank():
            return psum.tile([P, BANK], F32, tag="mx_sum", name="mx_sum", bufs=3)

        def copy_out(on_vector, out_ap, in_ap):
            if on_vector:
                nc.vector.tensor_copy(out=out_ap, in_=in_ap)
            else:
                nc.scalar.copy(out=out_ap, in_=in_ap)

        ident_f = keep.tile([P, P], F32)
        make_identity(nc, ident_f[:])
        ident_b = keep.tile([P, P], BF16)
        make_identity(nc, ident_b[:])
        ones_f = keep.tile([P, P], F32)
        nc.vector.memset(ones_f[:], 1.0)
        neg_half = keep.tile([P, KC], F32)
        nc.vector.memset(neg_half[:], -0.5)
        warm = keep.tile([P, 1], F32)
        nc.vector.memset(warm[:], 0.0)
        nc.scalar.activation(out=warm[:], in_=warm[:], func=ACT.Exp)

        xn_codes = [keep.tile([P, D], U32, name="xn_codes%d" % ch, align_bytes=256) for ch in range(CHUNKS)]
        xn_scales = [keep.tile([P, D], U8, name="xn_scales%d" % ch, align_bytes=256) for ch in range(CHUNKS)]
        c2T = keep.tile([P, KC, D], BF16)
        sums = keep.tile([P, 2, KC, CHUNKS], F32)
        sum_a = sums[:, 0]
        sum_aa = sums[:, 1]
        totals = keep.tile([P, 2, KC], F32)
        gamma_beta = keep.tile([P, 2 * KC], F32)
        spread = keep.tile([P, KC], F32)
        rstd = keep.tile([P, KC], F32)
        gamma_mean = keep.tile([P, KC], F32)
        bn_scale = keep.tile([P, KC], F32)
        bn_shift = keep.tile([P, KC], F32)
        neg_a_sum = keep.tile([P, B, KC], F32)

        a_sb = {}

        def a_view(ch, kc):
            return a_sb[ch, kc // 2][:, kc % 2, :]

        def normalise_group(ch, kc, on_vector):
            if on_vector:
                nc.vector.tensor_scalar(
                    out=a_view(ch, kc),
                    in0=a_view(ch, kc),
                    scalar1=bn_scale[:, kc : kc + 1],
                    scalar2=bn_shift[:, kc : kc + 1],
                    op0=ALU.mult,
                    op1=ALU.add,
                )
            else:
                nc.scalar.activation(
                    out=a_view(ch, kc),
                    in_=a_view(ch, kc),
                    func=ACT.Identity,
                    scale=bn_scale[:, kc : kc + 1],
                    bias=bn_shift[:, kc : kc + 1],
                )

        def normalise(ch, on_vector):
            for kc in range(KC):
                normalise_group(ch, kc, kc in on_vector)

        def normalise_scalar(ch):
            for kc in range(KC):
                if kc not in NV:
                    normalise_group(ch, kc, False)

        def normalise_vector(ch):
            for kc in NV:
                normalise_group(ch, kc, True)

        xn_grouped = {}

        def quantise_xn(ch):
            nc.vector.quantize_mx(
                out=xn_codes[ch][:].bitcast(FP8X4), scales=xn_scales[ch][:], in_=xn_grouped[ch][:]
            )

        with tc.tile_pool(name="stage1", bufs=2) as stage1:
            x_tiles = {}
            xd_grouped = {}
            xd_codes = {}
            xd_scales = {}
            X_BUFS = 4

            def load_chunk(ch, pieces=1):
                b, c = divmod(ch, CHUNKS_PER_BATCH)
                x_tiles[ch] = stage1.tile([P, PACK * D], BF16, tag="x_sb", name="x_sb", bufs=X_BUFS)
                rows = x[b, c * CHUNK : (c + 1) * CHUNK, :].rearrange("(q j) d -> q (j d)", j=PACK)
                span = PACK * D // pieces
                for first in range(0, PACK * D, span):
                    nc.sync.dma_start(
                        out=x_tiles[ch][:, first : first + span], in_=rows[:, first : first + span]
                    )

            def transpose_chunk(ch):
                x_words = x_tiles[ch][:].bitcast(F32)
                xd_grouped[ch] = stage1.tile(
                    [P, D_PASSES * CHUNK * PACK], BF16, tag="xd_grouped", name="xd_grouped", align_bytes=256
                )
                xd_words = xd_grouped[ch][:].bitcast(F32).rearrange("q (g n u) -> q g n u", g=D_PASSES, u=2)
                for j in range(PACK):
                    xt = transpose_bank([P, BANK], F32)
                    for h in range(2 * D_PASSES):
                        first = j * (D // 2) + h * P
                        nc.tensor.transpose(xt[:, h * P : (h + 1) * P], x_words[:, first : first + P], ident_f[:])
                    copy_out(
                        (ch, j) in V_XCP,
                        xd_words[:, :, j * P : (j + 1) * P, :],
                        xt[:].rearrange("q (g u n) -> q g n u", g=D_PASSES, u=2),
                    )

            def quantise_xd(ch):
                xd_codes[ch] = stage1.tile(
                    [P, D_PASSES * CHUNK], U32, tag="xd_codes", name="xd_codes", align_bytes=256
                )
                xd_scales[ch] = stage1.tile(
                    [P, D_PASSES * CHUNK], U8, tag="xd_scales", name="xd_scales", align_bytes=256
                )
                nc.vector.quantize_mx(
                    out=xd_codes[ch][:].bitcast(FP8X4), scales=xd_scales[ch][:], in_=xd_grouped[ch][:]
                )

            def first_matmul(ch):
                for kc in range(KC):
                    if kc % 2 == 0:
                        a_sb[ch, kc // 2] = wide.tile([P, 2, CHUNK], F32, tag="wide", name="a_sb")
                    acc = sum_bank()
                    for g in range(D_PASSES):
                        k_cols = slice(g * K + kc * P, g * K + (kc + 1) * P)
                        n_cols = slice(g * CHUNK, (g + 1) * CHUNK)
                        nc.tensor.matmul_mx(
                            out=acc[:],
                            lhsT=c_codes[:, k_cols].bitcast(FP8X4),
                            lhsT_scale=c_scales[:, k_cols],
                            rhs=xd_codes[ch][:, n_cols].bitcast(FP8X4),
                            rhs_scale=xd_scales[ch][:, n_cols],
                            start=(g == 0),
                            stop=(g == D_PASSES - 1),
                        )
                    squares = scrap.tile([P, D], BF16, tag="squares")
                    nc.scalar.activation(
                        out=a_view(ch, kc), in_=acc[:], func=ACT.Identity, accum_out=sum_a[:, kc, ch : ch + 1]
                    )
                    if ch == CHUNKS - 1:
                        if kc == KC - 1:
                            add_up(0)
                        nc.vector.scalar_tensor_tensor(
                            out=squares[:, 0:CHUNK],
                            in0=acc[:],
                            scalar=1.0,
                            in1=a_view(ch, kc),
                            op0=ALU.mult,
                            op1=ALU.mult,
                            accum_out=sum_aa[:, kc, ch : ch + 1],
                        )
                    else:
                        nc.scalar.activation(
                            out=squares[:, 0:CHUNK], in_=acc[:], func=ACT.Square, accum_out=sum_aa[:, kc, ch : ch + 1]
                        )

            def add_up(which):
                nc.vector.tensor_reduce(out=totals[:, which], in_=sums[:, which], axis=AXIS_X, op=ALU.add)

            def regroup_xn(ch, parts, on_vector=True):
                if parts.start == 0:
                    xn_grouped[ch] = scrap.tile(
                        [P, D * PACK], BF16, tag="xn_grouped", name="xn_grouped", align_bytes=256
                    )
                s = slice(parts.start * D // 16, parts.stop * D // 16)
                copy_out(
                    on_vector,
                    xn_grouped[ch][:].rearrange("q (s i j) -> q s j i", i=4, j=PACK)[:, s],
                    x_tiles[ch][:].rearrange("q (j s i) -> q s j i", j=PACK, i=4)[:, s],
                )

            c_raw = stage1.tile([P, 2 * D_PASSES, 2, K], BF16, bufs=1)
            for g in range(D_PASSES):
                nc.sync.dma_start(
                    out=c_raw[:, 2 * g : 2 * g + 2],
                    in_=clusters[g * K_PASS : (g + 1) * K_PASS].rearrange("(u q e) k -> q u e k", u=2, e=2),
                )
            load_chunk(0, 2)
            for ch in range(1, X_BUFS):
                load_chunk(ch)
            gb_rows = stage1.tile([P, P], BF16, bufs=1)
            nc.vector.memset(gb_rows[:], 0.0)
            nc.sync.dma_start(out=gb_rows[0:KC, :], in_=bn_gamma.rearrange("(r k) -> r k", k=P))
            nc.sync.dma_start(out=gb_rows[KC : 2 * KC, :], in_=bn_beta.rearrange("(r k) -> r k", k=P))

            c_grouped = stage1.tile([P, D_PASSES, K, PACK], BF16, bufs=1, align_bytes=256)
            c_codes = stage1.tile([P, D_PASSES * K], U32, bufs=1, align_bytes=256)
            c_scales = stage1.tile([P, D_PASSES * K], U8, bufs=1, align_bytes=256)

            def group_clusters(g):
                nc.vector.tensor_copy(
                    out=c_grouped[:, g].rearrange("q (s i) t -> q s t i", i=4),
                    in_=c_raw[:, 2 * g : 2 * g + 2].rearrange("q u e (s i) -> q s (u e) i", i=4),
                )

            def quantise_clusters(g):
                nc.vector.quantize_mx(
                    out=c_codes[:, g * K : (g + 1) * K].bitcast(FP8X4),
                    scales=c_scales[:, g * K : (g + 1) * K],
                    in_=c_grouped[:, g].rearrange("q k t -> q (k t)"),
                )

            transpose_chunk(0)
            regroup_xn(0, range(0, 1), on_vector=False)
            group_clusters(0)
            group_clusters(1)
            quantise_clusters(0)
            quantise_clusters(1)
            quantise_xd(0)

            for ch in range(CHUNKS):
                if ch + 1 < CHUNKS:
                    transpose_chunk(ch + 1)
                if ch == CHUNKS - 1:
                    gb_ps = transpose_bank([P, P], BF16)
                    nc.tensor.transpose(gb_ps[:], gb_rows[:], ident_b[:])
                    nc.vector.tensor_copy(out=gamma_beta[:], in_=gb_ps[:, 0 : 2 * KC])
                first_matmul(ch)
                if ch + 1 < CHUNKS:
                    regroup_xn(ch, range(1 if ch == 0 else 0, 4))
                    quantise_xd(ch + 1)
                    quantise_xn(ch)
                if ch + X_BUFS < CHUNKS:
                    load_chunk(ch + X_BUFS)

            c2_raw = stage1.tile([P, D_TILES, K], BF16, bufs=1)
            nc.sync.dma_start(out=c2_raw[:], in_=clusters2[0].rearrange("(t q) k -> q t k", q=P))
            for kc in range(KC):
                c2_ps = transpose_bank([P, D], BF16)
                for t in range(D_TILES):
                    nc.tensor.transpose(
                        c2_ps[:, t * P : (t + 1) * P], c2_raw[:, t, kc * P : (kc + 1) * P], ident_b[:]
                    )
                nc.scalar.copy(out=c2T[:, kc, :], in_=c2_ps[:])

            nc.vector.scalar_tensor_tensor(
                out=spread[:], in0=totals[:, 0], scalar=-1.0 / ROWS, in1=totals[:, 0], op0=ALU.mult, op1=ALU.mult
            )
            add_up(1)
            nc.vector.scalar_tensor_tensor(
                out=gamma_mean[:],
                in0=totals[:, 0],
                scalar=-ROOT_ROWS / ROWS,
                in1=gamma_beta[:, 0:KC],
                op0=ALU.mult,
                op1=ALU.mult,
            )
            nc.vector.tensor_tensor(out=spread[:], in0=spread[:], in1=totals[:, 1], op=ALU.add)
            nc.vector.tensor_scalar(
                out=spread[:], in0=spread[:], scalar1=0.0, scalar2=ROWS * BN_EPS, op0=ALU.max, op1=ALU.add
            )
            nc.gpsimd.tensor_tensor(out=rstd[:], in0=spread[:], in1=neg_half[:], op=ALU.pow)
            regroup_xn(CHUNKS - 1, range(0, 2))
            regroup_xn(CHUNKS - 1, range(2, 3), on_vector=False)
            nc.vector.tensor_tensor(out=bn_shift[:], in0=gamma_mean[:], in1=rstd[:], op=ALU.mult)
            nc.vector.scalar_tensor_tensor(
                out=bn_scale[:], in0=rstd[:], scalar=ROOT_ROWS, in1=gamma_beta[:, 0:KC], op0=ALU.mult, op1=ALU.mult
            )
            nc.vector.tensor_tensor(out=bn_shift[:], in0=gamma_beta[:, KC : 2 * KC], in1=bn_shift[:], op=ALU.add)

            normalise(0, (1, 3))
            regroup_xn(CHUNKS - 1, range(3, 4))

        stage2 = ctx.enter_context(tc.tile_pool(name="stage2", bufs=2, reuse_waits="tile"))
        zt = {}
        e = {}
        neg_max = {}
        row_sum = {}
        recip = {}
        p_grouped = {}
        p_codes = {}
        p_scales = {}
        a_sum_ps = {}

        def transpose_z(ch):
            for j in range(PACK):
                zt[ch, j] = transpose_bank([P, K], F32)
                for kc in range(KC):
                    nc.tensor.transpose(
                        zt[ch, j][:, kc * P : (kc + 1) * P], a_view(ch, kc)[:, j * P : (j + 1) * P], ident_f[:]
                    )

        def row_max(ch, j):
            if j == 0:
                neg_max[ch] = stage2.tile([P, PACK], F32, tag="neg_max", name="neg_max")
            nc.vector.tensor_reduce(
                out=neg_max[ch][:, j : j + 1], in_=zt[ch, j][:], axis=AXIS_X, op=ALU.max, negate=True
            )

        def exponentials(ch):
            e[ch] = stage2.tile([P, PACK, K], F32, tag="e", name="e", bufs=3)
            row_sum[ch] = stage2.tile([P, PACK], F32, tag="row_sum", name="row_sum")
            for j in range(PACK):
                nc.scalar.activation(
                    out=e[ch][:, j, :],
                    in_=zt[ch, j][:],
                    func=ACT.Exp,
                    bias=neg_max[ch][:, j : j + 1],
                    scale=1.0,
                    accum_out=row_sum[ch][:, j : j + 1],
                )

        def divide(ch):
            for j in range(PACK):
                nc.scalar.activation(
                    out=e[ch][:, j, :], in_=e[ch][:, j, :], func=ACT.Copy, scale=recip[ch][:, j : j + 1]
                )

        def sum_p(ch):
            b, c = divmod(ch, CHUNKS_PER_BATCH)
            if c == 0:
                a_sum_ps[b] = psum.tile([P, BANK], F32, tag="small", name="a_sum")
            for j in range(PACK):
                for kc in range(KC):
                    nc.tensor.matmul(
                        out=a_sum_ps[b][:, kc * P : (kc + 1) * P],
                        lhsT=e[ch][:, j, kc * P : (kc + 1) * P],
                        rhs=ident_f[:],
                        is_transpose=True,
                        start=(c == 0 and j == 0 and kc == 0),
                        stop=(c == CHUNKS_PER_BATCH - 1 and j == PACK - 1 and kc == KC - 1),
                    )

        def negate_a_sum(b):
            if b == B - 1:
                for kc in range(KC):
                    addends = scrap.tile([P, D], BF16, tag="squares", name="addends")
                    nc.scalar.activation(
                        out=addends[:, 0:P],
                        in_=a_sum_ps[b][:, kc * P : (kc + 1) * P],
                        func=ACT.Copy,
                        scale=-1.0,
                        accum_out=neg_a_sum[:, b, kc : kc + 1],
                    )
                return
            nc.vector.tensor_reduce(
                out=neg_a_sum[:, b, :],
                in_=a_sum_ps[b][:].rearrange("k (kc n) -> k kc n", kc=KC),
                axis=AXIS_X,
                op=ALU.add,
                negate=True,
            )

        def round_p(ch):
            p_grouped[ch] = stage2.tile([P, K, PACK], BF16, tag="p_grouped", name="p_grouped", align_bytes=256)
            nc.vector.tensor_copy(
                out=p_grouped[ch][:].rearrange("q (s i) j -> q s j i", i=4),
                in_=e[ch][:].rearrange("q j (s i) -> q s j i", i=4),
            )

        def quantise_p(ch):
            p_codes[ch] = stage2.tile([P, K], U32, tag="p_codes", name="p_codes", bufs=CHUNKS, align_bytes=256)
            p_scales[ch] = stage2.tile([P, K], U8, tag="p_scales", name="p_scales", bufs=CHUNKS, align_bytes=256)
            nc.vector.quantize_mx(
                out=p_codes[ch][:].bitcast(FP8X4),
                scales=p_scales[ch][:],
                in_=p_grouped[ch][:].rearrange("q k j -> q (k j)"),
            )

        v = {}
        sum_vv = {}
        floored = {}
        unit = {}
        unit_sum = {}
        total_ps = {}
        factor = {}
        out_rows = {}
        HALF_TILES = D_TILES // 2

        def second_matmul(b, kc):
            v[b, kc] = wide.tile([P, D], F32, tag="wide", name="v")
            for half in range(D // BANK):
                d_cols = slice(half * BANK, (half + 1) * BANK)
                acc = sum_bank()
                for c in range(CHUNKS_PER_BATCH):
                    ch = b * CHUNKS_PER_BATCH + c
                    k_cols = slice(kc * P, (kc + 1) * P)
                    nc.tensor.matmul_mx(
                        out=acc[:],
                        lhsT=p_codes[ch][:, k_cols].bitcast(FP8X4),
                        lhsT_scale=p_scales[ch][:, k_cols],
                        rhs=xn_codes[ch][:, d_cols].bitcast(FP8X4),
                        rhs_scale=xn_scales[ch][:, d_cols],
                        start=(c == 0),
                        stop=(c == CHUNKS_PER_BATCH - 1),
                    )
                nc.vector.scalar_tensor_tensor(
                    out=v[b, kc][:, d_cols],
                    in0=c2T[:, kc, d_cols],
                    scalar=neg_a_sum[:, b, kc : kc + 1],
                    in1=acc[:],
                    op0=ALU.mult,
                    op1=ALU.add,
                )

        def square_sum(b, kc):
            if kc == 0:
                sum_vv[b] = stage2.tile([P, KC], F32, tag="sum_vv", name="sum_vv")
            squares = scrap.tile([P, D], BF16, tag="squares")
            nc.scalar.activation(out=squares[:], in_=v[b, kc][:], func=ACT.Square, accum_out=sum_vv[b][:, kc : kc + 1])

        def unit_norms(b):
            unit[b] = stage2.tile([P, KC], F32, tag="unit", name="unit")
            floored[b] = stage2.tile([P, KC], F32, tag="floored", name="floored")
            nc.vector.tensor_scalar(
                out=unit[b][:],
                in0=sum_vv[b][:],
                scalar1=1.0 / (NORM_EPS * NORM_EPS),
                scalar2=1.0,
                op0=ALU.mult,
                op1=ALU.min,
            )
            nc.vector.tensor_scalar(
                out=floored[b][:], in0=sum_vv[b][:], scalar1=NORM_EPS * NORM_EPS, scalar2=None, op0=ALU.max
            )
            unit_sum[b] = stage2.tile([P, 1], F32, tag="unit_sum", name="unit_sum")
            nc.vector.tensor_reduce(out=unit_sum[b][:], in_=unit[b][:], axis=AXIS_X, op=ALU.add)
            if b == B - 1:
                nc.gpsimd.tensor_tensor(out=own_norm[:], in0=floored[b][:], in1=neg_half[:], op=ALU.pow)

        own_norm = keep.tile([P, KC], F32)
        row_norm = keep.tile([P, 1], F32)

        def invert_row_norm(b):
            nc.vector.tensor_scalar(
                out=row_norm[:], in0=total_ps[b][:], scalar1=NORM_EPS * NORM_EPS, scalar2=None, op0=ALU.max
            )
            nc.gpsimd.tensor_tensor(out=row_norm[:], in0=row_norm[:], in1=neg_half[:, 0:1], op=ALU.pow)

        def add_over_partitions(b):
            total_ps[b] = psum.tile([P, 1], F32, tag="small", name="total")
            nc.tensor.matmul(out=total_ps[b][:], lhsT=ones_f[:], rhs=unit_sum[b][:], start=True, stop=True)

        def make_factor(b):
            factor[b] = stage2.tile([P, KC], F32, tag="factor", name="factor")
            nc.vector.scalar_tensor_tensor(
                out=factor[b][:],
                in0=total_ps[b][:].to_broadcast([P, KC]),
                scalar=NORM_EPS * NORM_EPS,
                in1=floored[b][:],
                op0=ALU.max,
                op1=ALU.mult,
            )
            nc.gpsimd.tensor_tensor(out=factor[b][:], in0=factor[b][:], in1=neg_half[:], op=ALU.pow)

        def scale_v(b, kc):
            nc.vector.tensor_scalar(
                out=v[b, kc][:], in0=v[b, kc][:], scalar1=factor[b][:, kc : kc + 1], scalar2=None, op0=ALU.mult
            )

        def dram_tiles(b):
            return out[b].rearrange("(t q k) -> q t k", q=P, k=K)

        def transpose_group(b, dg, kc, on_vector):
            if kc == 0:
                out_rows[b, dg] = stage2.tile([P, HALF_TILES, K], F32, tag="out_rows", name="out_rows", bufs=4)
            vt = transpose_bank([P, HALF_TILES, P], F32)
            for t in range(HALF_TILES):
                first = (dg * HALF_TILES + t) * P
                nc.tensor.transpose(vt[:, t, :], v[b, kc][:, first : first + P], ident_f[:])
            copy_out(on_vector, out_rows[b, dg][:, :, kc * P : (kc + 1) * P], vt[:])
            if kc == KC - 1:
                tiles = slice(dg * HALF_TILES, (dg + 1) * HALF_TILES)
                nc.sync.dma_start(out=dram_tiles(b)[:, tiles, :], in_=out_rows[b, dg][:])

        def scale_own(kc, on_vector):
            v_last = v[B - 1, kc][:]
            if on_vector:
                nc.vector.tensor_scalar(
                    out=v_last, in0=v_last, scalar1=own_norm[:, kc : kc + 1], scalar2=None, op0=ALU.mult
                )
            else:
                nc.scalar.activation(out=v_last, in_=v_last, func=ACT.Copy, scale=own_norm[:, kc : kc + 1])

        def transpose_tile(b, t, on_vector):
            dg, tt = divmod(t, HALF_TILES)
            if tt == 0:
                out_rows[b, dg] = stage2.tile([P, HALF_TILES, K], F32, tag="out_rows", name="out_rows", bufs=4)
            vt = transpose_bank([P, K], F32)
            for kc in range(KC):
                nc.tensor.transpose(vt[:, kc * P : (kc + 1) * P], v[b, kc][:, t * P : (t + 1) * P], ident_f[:])
            if on_vector:
                nc.vector.tensor_scalar(
                    out=out_rows[b, dg][:, tt, :], in0=vt[:], scalar1=row_norm[:, 0:1], scalar2=None, op0=ALU.mult
                )
            else:
                nc.scalar.activation(out=out_rows[b, dg][:, tt, :], in_=vt[:], func=ACT.Copy, scale=row_norm[:, 0:1])
            if tt % STORE_TILES == STORE_TILES - 1:
                ts = slice(t - STORE_TILES + 1, t + 1)
                nc.sync.dma_start(
                    out=dram_tiles(b)[:, ts, :], in_=out_rows[b, dg][:, tt - STORE_TILES + 1 : tt + 1, :]
                )

        transpose_z(0)
        for kc in (0, 1, 2):
            normalise_group(1, kc, False)
        for j in range(PACK):
            row_max(0, j)
        for kc in (3,):
            normalise_group(1, kc, True)
        quantise_xn(CHUNKS - 1)
        for ch in range(CHUNKS + 1):
            if ch < CHUNKS:
                if ch > 0:
                    for j in range(PACK):
                        row_max(ch, j)
                exponentials(ch)
            if ch + 2 < CHUNKS:
                normalise_scalar(ch + 2)
            if ch > 0:
                round_p(ch - 1)
            if ch < CHUNKS:
                recip[ch] = stage2.tile([P, PACK], F32, tag="recip", name="recip", bufs=3)
                nc.vector.reciprocal(out=recip[ch][:], in_=row_sum[ch][:])
                divide(ch)
            if ch + 1 < CHUNKS:
                transpose_z(ch + 1)
            if ch > 0 and ch % CHUNKS_PER_BATCH == 0:
                negate_a_sum(ch // CHUNKS_PER_BATCH - 1)
            if ch == CHUNKS - 1:
                for kc in range(EARLY):
                    second_matmul(0, kc)
            if ch < CHUNKS:
                sum_p(ch)
            if ch + 2 < CHUNKS:
                normalise_vector(ch + 2)
            if ch > 0:
                quantise_p(ch - 1)
            if ch == CHUNKS - 1:
                for kc in range(EARLY):
                    square_sum(0, kc)

        def out_unit(b, unit):
            dg, half = divmod(unit, 2)
            transpose_group(b, dg, 2 * half, unit == 2)
            transpose_group(b, dg, 2 * half + 1, False)

        OUT_LAG = 2 * KC - 1
        for step in range(EARLY, B * KC):
            b, kc = divmod(step, KC)
            second_matmul(b, kc)
            if b > 0 and kc == 1:
                add_over_partitions(b - 1)
            if step >= OUT_LAG:
                out_unit(*divmod(step - OUT_LAG, KC))
            square_sum(b, kc)
            if b > 0 and kc == 0:
                unit_norms(b - 1)
            if b > 0 and kc == 1:
                make_factor(b - 1)
            ahead = step + 1 - OUT_LAG
            if ahead >= 0 and ahead % KC < 2:
                scale_v(ahead // KC, 2 * (ahead % KC))
                scale_v(ahead // KC, 2 * (ahead % KC) + 1)
        before, last = B - 2, B - 1
        unit_norms(last)
        for kc in (2, 3):
            transpose_group(before, 0, kc, False)
        add_over_partitions(last)
        transpose_group(before, 1, 0, True)
        invert_row_norm(last)
        transpose_group(before, 1, 1, True)
        transpose_group(before, 1, 2, False)
        transpose_group(before, 1, 3, False)
        scale_own(0, True)
        scale_own(2, False)
        scale_own(1, True)
        scale_own(3, True)
        for t in range(D_TILES):
            transpose_tile(last, t, t % 2 == 0)
